import numpy as np
import ml_dtypes


def mxq(x, axis, fmt="e4m3"):
    dtype, down = {"e4m3": (ml_dtypes.float8_e4m3fn, 7), "e5m2": (ml_dtypes.float8_e5m2, 14)}[fmt]
    v = np.moveaxis(np.asarray(x, np.float32).astype(ml_dtypes.bfloat16).astype(np.float64), axis, -1)
    blocks = v.reshape(v.shape[:-1] + (-1, 32))
    amax = np.abs(blocks).max(-1, keepdims=True)
    byte = np.maximum(np.where(amax > 0, np.frexp(amax)[1] - 1 + 127, 0) - down, 1)
    scale = np.exp2(byte - 127.0)
    codes = (blocks / scale).astype(np.float32).astype(dtype).astype(np.float64)
    return np.moveaxis((codes * scale).reshape(v.shape), -1, axis)


WIDE = False


def mx_kscale(k):
    if not WIDE:
        return np.ones(k)
    levels = np.array([10, -10, 5, -5, 0])
    if k % 512:
        return np.exp2(np.random.permutation(np.resize(levels, k // 32))).repeat(32)
    a = np.empty((k // 512, 16))
    for p in range(k // 512):
        a[p, :8] = np.random.permutation(np.resize(levels, 8))
        for g in range(8):
            far = levels[np.abs(levels - a[p, g]) >= 10]
            a[p, g + 8] = far[np.random.randint(len(far))]
    return np.exp2(a.ravel()).repeat(32)


BF16 = ml_dtypes.bfloat16


def bf(x):
    return np.asarray(x, np.float32).astype(BF16)


def f64(x):
    return np.asarray(x).astype(np.float64)


NB, DI, DO, B = 8, 1024, 1024, 256
F = NB * DO
EPS = 1e-5


def draw0():
    s, t = mx_kscale(DI), mx_kscale(F)
    tk = t.reshape(NB, DO)
    return {"x": bf(np.random.standard_normal((B, DI)) * s),
            "W": bf(np.random.standard_normal((NB, DI, DO)) / np.sqrt(DI) / s[None, :, None]),
            "b": bf(np.random.standard_normal((NB, DO)) * 0.5),
            "gamma": bf((1.0 + 0.2 * np.random.standard_normal((NB, DO))) * tk),
            "beta": bf(0.2 * np.random.standard_normal((NB, DO)) * tk),
            "Wf1": bf(np.random.standard_normal((F, DO)) / np.sqrt(F) / t[:, None]),
            "bf1": bf(np.random.standard_normal(DO) * 0.3)}


def core(x, W, b, gamma, beta, Wf1, bf1):
    w2 = f64(W).transpose(1, 0, 2).reshape(DI, F)
    h = (mxq(f64(x), 1, "e4m3") @ mxq(w2, 0, "e4m3")).reshape(B, NB, DO) + f64(b)[None]
    h = np.maximum(h, 0.0)
    mean = h.mean(axis=0, keepdims=True)
    var = ((h - mean) ** 2).mean(axis=0, keepdims=True)
    h = (h - mean) * (1.0 / np.sqrt(var + EPS)) * f64(gamma)[None] + f64(beta)[None]
    fused = h.reshape(B, F)
    return np.maximum((mxq(fused, 1, "e4m3") @ mxq(f64(Wf1), 0, "e4m3")) + f64(bf1), 0.0)


def e4m3fn_bytes(y):
    return np.clip(np.asarray(y, np.float64), -448.0, 448.0).astype(np.float32).astype(ml_dtypes.float8_e4m3fn).view(np.uint8)


def e4m3fn_values(b):
    return np.asarray(b, np.uint8).view(ml_dtypes.float8_e4m3fn).astype(np.float64)


def setup_inputs():
    d = draw0()
    x0 = np.asarray(d['Wf1']).astype(np.float64)
    s = (np.max(np.abs(x0), axis=(1,), keepdims=True) / 448.0).astype(np.float32)
    out = {}
    for k, v in d.items():
        if k == 'Wf1':
            out['Wf1_bytes'] = e4m3fn_bytes(x0 / s.astype(np.float64))
            out['Wf1_scale'] = s
        else:
            out[k] = v
    return out


def reference(x, W, b, gamma, beta, Wf1_bytes, Wf1_scale, bf1):
    return core(x, W, b, gamma, beta, e4m3fn_values(Wf1_bytes) * Wf1_scale.astype(np.float64), bf1)

@@ -1,0 +1,361 @@
+from contextlib import ExitStack
+
+import concourse.mybir as mybir
+from concourse.masks import make_identity
+
+BRANCHES, D_IN, D_OUT, ROWS = 8, 1024, 1024, 256
+EPS = 1e-5
+FLOPS = 2 * ROWS * BRANCHES * D_OUT * (D_IN + D_OUT)
+
+F32 = mybir.dt.float32
+BF16 = mybir.dt.bfloat16
+U32 = mybir.dt.uint32
+U8 = mybir.dt.uint8
+FP8 = mybir.dt.float8_e4m3fn
+FP8X4 = mybir.dt.float8_e4m3fn_x4
+ACT = mybir.ActivationFunctionType
+ALU = mybir.AluOpType
+ENG = mybir.EngineType
+
+P = 128
+N_PI = (2, 1)
+
+
+def tile_extremeoptimizationlayer_pa_kernel(tc, x, W, b, gamma, beta, Wf1_bytes, Wf1_scale, bf1, out):
+    nc = tc.nc
+    with ExitStack() as ctx:
+        keep = ctx.enter_context(tc.tile_pool(name="keep", bufs=1))
+        wpool = ctx.enter_context(tc.tile_pool(name="wpool", bufs=1))
+        fpool = ctx.enter_context(tc.tile_pool(name="fpool", bufs=1))
+        hpool = ctx.enter_context(tc.tile_pool(name="hpool", bufs=1))
+        opool = ctx.enter_context(tc.tile_pool(name="opool", bufs=4))
+        accp = ctx.enter_context(tc.psum_pool(name="accp", bufs=1))
+        s1p = ctx.enter_context(tc.psum_pool(name="s1p", bufs=2))
+        pip = ctx.enter_context(tc.psum_pool(name="pip", bufs=2))
+
+        wraw, wgrp, wcod, wscl = {}, {}, {}, {}
+        fraw, fwid, fgrp, fcod, fscl = {}, {}, {}, {}, {}
+        act, nrm, ugrp, ucod, uscl = {}, {}, {}, {}, {}
+        pib, s1b = {}, {}
+        stats, small = {}, {}
+
+        def load_w(i, kg):
+            r = wpool.tile([P, 4, D_OUT], BF16, name="wraw", bufs=4, align_bytes=64)
+            wraw[i, kg] = r
+            v = W[i, kg * 512:(kg + 1) * 512, :].rearrange("(p j) n -> p j n", j=4)
+            if i == 0 and kg == 0:
+                nc.sync.dma_start(out=r[:, :, 0:512], in_=v[:, :, 0:512])
+            else:
+                nc.sync.dma_start(out=r[:], in_=v)
+
+        def load_f(i, g):
+            s = 2 * i + g
+            r = fpool.tile([P, 4, D_OUT], U8, name="fraw", bufs=5, align_bytes=64)
+            fraw[i, g] = r
+            nc.sync.dma_start(out=r[:], in_=Wf1_bytes[s * 512:(s + 1) * 512, :].rearrange("(p t) n -> p t n", t=4))
+
+        def pe_interleave(i, kg, blk):
+            if blk == 0:
+                wgrp_of(i, kg)
+            n0 = D_OUT - 256 * (N_PI[kg] - blk)
+            bank = pip.tile([P, 4, 64, 4], BF16, name="pi", tag="pi")
+            pib[i, kg, blk] = bank
+            v = wraw[i, kg][:, :, n0:n0 + 256].rearrange("p j (m t) -> p t m j", t=4)
+            for th in range(2):
+                nc.tensor.matmul(out=bank[:, 2 * th:2 * th + 2, :, :].rearrange("p t m j -> p (t m j)"), lhsT=ident_b[:],
+                                 rhs=v[:, 2 * th:2 * th + 2], start=True, stop=True)
+
+        def pe_exit(i, kg, blk):
+            m0 = 256 - 64 * (N_PI[kg] - blk)
+            nc.scalar.copy(out=wgrp[i, kg][:, :, m0:m0 + 64, :].rearrange("p t m j -> p t (m j)"),
+                           in_=pib[i, kg, blk][:].rearrange("p t m j -> p t (m j)"))
+
+        def wgrp_of(i, kg):
+            if (i, kg) not in wgrp:
+                wg = wpool.tile([P, 4, 256, 4], BF16, name="wgrp", bufs=3, align_bytes=64)
+                wgrp[i, kg] = wg
+            return wgrp[i, kg]
+
+        def w_interleave(i, kg):
+            n1 = D_OUT - 256 * N_PI[kg]
+            g = wgrp_of(i, kg)
+            nc.vector.tensor_copy(
+                out=g[:, :, 0:n1 // 4, :].rearrange("p t (c m) j -> p c t m j", m=2),
+                in_=wraw[i, kg][:, :, 0:n1].rearrange("p j (c m t) -> p c t m j", m=2, t=4))
+
+        def w_quant(i, kg):
+            c = wpool.tile([P, D_OUT], U32, name="wcod", bufs=4, align_bytes=64)
+            s = wpool.tile([P, D_OUT], U8, name="wscl", bufs=4, align_bytes=64)
+            wcod[i, kg], wscl[i, kg] = c, s
+            nc.vector.quantize_mx(out=c[:].bitcast(FP8X4), scales=s[:],
+                                  in_=wgrp[i, kg][:].rearrange("p t m j -> p (t m j)"))
+
+        def mm1(i, bk):
+            g, th = divmod(bk, 2)
+            bank = s1p.tile([P, 2, ROWS], F32, name="s1", tag="s1")
+            s1b[i, bk] = bank
+            for u in range(2):
+                t = 2 * th + u
+                cols = slice(t * 256 + g * 128, t * 256 + g * 128 + 128)
+                for kg in range(2):
+                    nc.tensor.matmul_mx(out=bank[:, u, :],
+                                        lhsT=wcod[i, kg][:, cols].bitcast(FP8X4), lhsT_scale=wscl[i, kg][:, cols],
+                                        rhs=xcod[:, kg * 256:(kg + 1) * 256].bitcast(FP8X4),
+                                        rhs_scale=xscl[:, kg * 256:(kg + 1) * 256],
+                                        start=(kg == 0), stop=(kg == 1))
+
+        def relu(i, bk):
+            g, th = divmod(bk, 2)
+            if th == 0:
+                a = hpool.tile([P, 4, ROWS], F32, name="act", bufs=4, align_bytes=64)
+                act[i, g] = a
+            for u in range(2):
+                t = 2 * th + u
+                nc.scalar.activation(out=act[i, g][:, t, :], in_=s1b[i, bk][:, u, :], func=ACT.Relu,
+                                     bias=prm[:, t, 2 * i + g:2 * i + g + 1])
+
+        def bn(i, g):
+            if g == 0:
+                st = hpool.tile([P, 4, 2, 6], F32, name="st", bufs=2)
+                stats[i] = st
+            for t in range(4):
+                nc.vector.bn_stats(out=stats[i][:, t, g, :], in_=act[i, g][:, t, :])
+
+        def sm(i, name, shape=(4, 2)):
+            tl = hpool.tile([P] + list(shape), F32, name="sm_" + name, bufs=2)
+            small[i, name] = tl
+            return tl
+
+        def st_sums(i):
+            st = stats[i]
+            sv = sm(i, "sv", (4, 2, 2))
+            nc.vector.tensor_tensor(out=sv[:], in0=st[:, :, :, 1:3], in1=st[:, :, :, 4:6], op=ALU.add)
+            dm = sm(i, "dm")
+            nc.vector.tensor_tensor(out=dm[:], in0=st[:, :, :, 1], in1=st[:, :, :, 4], op=ALU.subtract)
+
+        def st_d2(i):
+            d2 = sm(i, "d2")
+            dm = small[i, "dm"]
+            nc.vector.scalar_tensor_tensor(out=d2[:], in0=dm[:], scalar=0.25, in1=dm[:], op0=ALU.mult, op1=ALU.mult)
+
+        def st_var(i):
+            var = sm(i, "var")
+            nc.vector.scalar_tensor_tensor(out=var[:], in0=small[i, "sv"][:, :, :, 1], scalar=1.0 / 256, in1=small[i, "d2"][:],
+                                           op0=ALU.mult, op1=ALU.add)
+
+        def st_sqrt(i):
+            sd = sm(i, "sd")
+            nc.scalar.activation(out=sd[:], in_=small[i, "var"][:], func=ACT.Sqrt, bias=EPS)
+
+        def st_recip(i):
+            rs = sm(i, "rs")
+            nc.vector.reciprocal(out=rs[:], in_=small[i, "sd"][:])
+
+        def st_scale(i):
+            sc = sm(i, "sc")
+            nc.vector.tensor_tensor(out=sc[:], in0=small[i, "rs"][:], in1=prm[:, :, 16 + 2 * i:18 + 2 * i], op=ALU.mult)
+
+        def st_ms(i):
+            ms = sm(i, "ms")
+            nc.vector.scalar_tensor_tensor(out=ms[:], in0=small[i, "sv"][:, :, :, 0], scalar=-0.5, in1=small[i, "sc"][:],
+                                           op0=ALU.mult, op1=ALU.mult)
+
+        def st_shift(i):
+            sh = sm(i, "sh")
+            nc.vector.tensor_tensor(out=sh[:], in0=small[i, "ms"][:], in1=prm[:, :, 32 + 2 * i:34 + 2 * i], op=ALU.add)
+
+        def norm(i, g):
+            n = hpool.tile([P, 4, ROWS], BF16, name="nrm", bufs=3, align_bytes=64)
+            nrm[i, g] = n
+            for t in range(4):
+                nc.scalar.activation(out=n[:, t, :], in_=act[i, g][:, t, :], func=ACT.Identity,
+                                     scale=small[i, "sc"][:, t, g:g + 1], bias=small[i, "sh"][:, t, g:g + 1])
+
+        def u_interleave(i, g):
+            u = hpool.tile([P, 4 * ROWS], BF16, name="ugrp", bufs=3, align_bytes=64)
+            ugrp[i, g] = u
+            nc.vector.tensor_copy(out=u[:].rearrange("p (c i t) -> p c t i", i=4, t=4),
+                                  in_=nrm[i, g][:].rearrange("p t (c i) -> p c t i", i=4))
+
+        def u_quant(i, g):
+            c = hpool.tile([P, ROWS], U32, name="ucod", bufs=3, align_bytes=64)
+            s = hpool.tile([P, ROWS], U8, name="uscl", bufs=3, align_bytes=64)
+            ucod[i, g], uscl[i, g] = c, s
+            nc.vector.quantize_mx(out=c[:].bitcast(FP8X4), scales=s[:], in_=ugrp[i, g][:])
+
+        def f_widen(i, g, ts):
+            if ts[0] == 0:
+                w = fpool.tile([P, 4, D_OUT], BF16, name="fwid", bufs=3, align_bytes=64)
+                fwid[i, g] = w
+            s = 2 * i + g
+            for t in ts:
+                nc.scalar.activation(out=fwid[i, g][:, t, :], in_=fraw[i, g][:, t, :].bitcast(FP8), func=ACT.Copy,
+                                     scale=scl[:, t, s:s + 1])
+
+        def f_interleave(i, g, h):
+            if h == 0:
+                f = fpool.tile([P, 4 * D_OUT], BF16, name="fgrp", bufs=2, align_bytes=64)
+                fgrp[i, g] = f
+            nc.vector.tensor_copy(
+                out=fgrp[i, g][:, h * 2048:(h + 1) * 2048].rearrange("p (c i t) -> p c t i", i=4, t=4),
+                in_=fwid[i, g][:, :, h * 512:(h + 1) * 512].rearrange("p t (c i) -> p c t i", i=4))
+
+        def f_quant(i, g, h):
+            if h == 0:
+                c = fpool.tile([P, D_OUT], U32, name="fcod", bufs=3, align_bytes=64)
+                s = fpool.tile([P, D_OUT], U8, name="fscl", bufs=3, align_bytes=64)
+                fcod[i, g], fscl[i, g] = c, s
+            cols = slice(h * 512, (h + 1) * 512)
+            nc.vector.quantize_mx(out=fcod[i, g][:, cols].bitcast(FP8X4), scales=fscl[i, g][:, cols],
+                                  in_=fgrp[i, g][:, h * 2048:(h + 1) * 2048])
+
+        def mm2(i, g):
+            first, last = (i == 0 and g == 0), (i == BRANCHES - 1 and g == 1)
+            for h in range(2):
+                for rt in range(2):
+                    rows, cols = slice(rt * 128, (rt + 1) * 128), slice(h * 512, (h + 1) * 512)
+                    nc.tensor.matmul_mx(out=acc[h, rt][:],
+                                        lhsT=ucod[i, g][:, rows].bitcast(FP8X4), lhsT_scale=uscl[i, g][:, rows],
+                                        rhs=fcod[i, g][:, cols].bitcast(FP8X4), rhs_scale=fscl[i, g][:, cols],
+                                        start=first, stop=last)
+
+        prow = keep.tile([P, 512], BF16, name="prow", align_bytes=64)
+        srow = keep.tile([P, 512], F32, name="srow", align_bytes=64)
+        ident_f = keep.tile([P, P], F32, name="ident_f", align_bytes=64)
+        ident_b = keep.tile([P, P], BF16, name="ident_b", align_bytes=64)
+        dummy = keep.tile([P, 1], F32, name="dummy")
+        dummy2 = keep.tile([P, 1], F32, name="dummy2")
+        nc.vector.memset(srow[:], 0.0)
+        nc.vector.memset(prow[:], 0.0)
+        nc.vector.memset(dummy[:], 1.0)
+        make_identity(nc, ident_f[:])
+        make_identity(nc, ident_b[:])
+        xs = []
+        load_w(0, 0)
+        for rt in range(2):
+            xt = keep.tile([P, D_IN], BF16, name="xs" + str(rt), align_bytes=64)
+            xs.append(xt)
+            nc.sync.dma_start(out=xt[:], in_=x[rt * 128:(rt + 1) * 128, :])
+        nc.sync.dma_start(out=wraw[0, 0][:, :, 512:1024],
+                          in_=W[0, 0:512, 512:1024].rearrange("(p j) n -> p j n", j=4))
+        load_f(0, 0)
+        load_w(0, 1)
+        load_f(0, 1)
+        nc.scalar.dma_start(out=srow[0:16, :], in_=Wf1_scale.rearrange("(s c) o -> s (o c)", c=512))
+        nc.scalar.dma_start(out=prow[0:16, :], in_=b.rearrange("k (g c) -> (k g) c", c=512))
+        nc.scalar.dma_start(out=prow[16:32, :], in_=gamma.rearrange("k (g c) -> (k g) c", c=512))
+        nc.scalar.dma_start(out=prow[32:48, :], in_=beta.rearrange("k (g c) -> (k g) c", c=512))
+        nc.scalar.activation(out=dummy2[:], in_=dummy[:], func=ACT.Sqrt)
+
+        scl = keep.tile([P, 4, 16], F32, name="scl")
+        prm = keep.tile([P, 4, 48], F32, name="prm")
+        xgrp = keep.tile([P, 2, 1024], BF16, name="xgrp", align_bytes=64)
+        xcod = keep.tile([P, 512], U32, name="xcod", align_bytes=64)
+        xscl = keep.tile([P, 512], U8, name="xscl", align_bytes=64)
+        bf1b = keep.tile([P, D_OUT], BF16, name="bf1b", align_bytes=64)
+        acc = {}
+        for h in range(2):
+            for rt in range(2):
+                a = accp.tile([P, 512], F32, name="acc" + str(2 * h + rt))
+                acc[h, rt] = a
+
+        with tc.manual_schedule(engines={ENG.PE, ENG.Activation, ENG.DVE, ENG.SP}):
+            ps = s1p.tile([P, 4, 128], F32, name="ps", tag="s1")
+            for t in range(4):
+                nc.tensor.transpose(ps[:, t, :], srow[:, t:512:4], ident_f[:])
+            nc.scalar.copy(out=scl[:], in_=ps[:, :, 0:16])
+            for kg in range(2):
+                xp = s1p.tile([P, 2, ROWS], F32, name="xp", tag="s1")
+                for rt in range(2):
+                    for u in range(2):
+                        nc.tensor.transpose(xp[:, u, rt * 128:(rt + 1) * 128],
+                                            xs[rt][:].bitcast(F32)[:, 256 * kg + u:256 * (kg + 1):2], ident_f[:])
+                nc.scalar.copy(out=xgrp[:, kg, :].bitcast(F32).rearrange("p (r u) -> p r u", u=2),
+                               in_=xp[:].rearrange("p u r -> p r u"))
+            pp = pip.tile([P, 4, 128], BF16, name="pp", tag="pi")
+            for t in range(4):
+                nc.tensor.transpose(pp[:, t, :], prow[:, t:512:4], ident_b[:])
+            nc.scalar.copy(out=prm[:], in_=pp[:, :, 0:48])
+
+            for i in range(-1, BRANCHES):
+                cur, nxt = i >= 0, i + 1 < BRANCHES
+                if i + 2 < BRANCHES:
+                    load_w(i + 2, 0)
+                    load_f(i + 2, 0)
+                    load_w(i + 2, 1)
+                    load_f(i + 2, 1)
+                if i == 1:
+                    nc.sync.dma_start(out=bf1b[:], in_=bf1.partition_broadcast(128))
+                if cur:
+                    mm1(i, 0)
+                    mm1(i, 1)
+                if nxt:
+                    pe_interleave(i + 1, 0, 0)
+                    pe_interleave(i + 1, 0, 1)
+                    w_interleave(i + 1, 0)
+                if cur:
+                    relu(i, 0)
+                    relu(i, 1)
+                    mm1(i, 2)
+                    mm1(i, 3)
+                    relu(i, 2)
+                    relu(i, 3)
+                    bn(i, 0)
+                if nxt:
+                    pe_exit(i + 1, 0, 0)
+                    pe_exit(i + 1, 0, 1)
+                    pe_interleave(i + 1, 1, 0)
+                if cur:
+                    bn(i, 1)
+                    if i > 0:
+                        mm2(i - 1, 1)
+                if i == -1:
+                    nc.vector.quantize_mx(out=xcod[:].bitcast(FP8X4), scales=xscl[:],
+                                          in_=xgrp[:].rearrange("p k c -> p (k c)"))
+                if nxt:
+                    w_quant(i + 1, 0)
+                if cur:
+                    st_sums(i)
+                if nxt:
+                    w_interleave(i + 1, 1)
+                if cur:
+                    f_widen(i, 1, (0, 1, 2, 3))
+                    st_d2(i)
+                    f_interleave(i, 0, 0)
+                    st_var(i)
+                    f_interleave(i, 0, 1)
+                    st_sqrt(i)
+                if nxt:
+                    pe_exit(i + 1, 1, 0)
+                    f_widen(i + 1, 0, (0, 1, 2))
+                if cur:
+                    st_recip(i)
+                    f_quant(i, 0, 0)
+                    st_scale(i)
+                    f_quant(i, 0, 1)
+                    st_ms(i)
+                    f_interleave(i, 1, 0)
+                    st_shift(i)
+                    f_interleave(i, 1, 1)
+                    norm(i, 0)
+                    norm(i, 1)
+                if nxt:
+                    f_widen(i + 1, 0, (3,))
+                    w_quant(i + 1, 1)
+                if cur:
+                    u_interleave(i, 0)
+                    u_interleave(i, 1)
+                    u_quant(i, 0)
+                    mm2(i, 0)
+                    u_quant(i, 1)
+                    f_quant(i, 1, 0)
+                    f_quant(i, 1, 1)
+            mm2(BRANCHES - 1, 1)
+
+            for h in range(2):
+                for rt in range(2):
+                    s = opool.tile([P, 512], F32, name="osum", align_bytes=64)
+                    o = opool.tile([P, 512], F32, name="ores", align_bytes=64)
+                    nc.vector.tensor_tensor(out=s[:], in0=acc[h, rt][:], in1=bf1b[:, h * 512:(h + 1) * 512], op=ALU.add)
+                    nc.scalar.activation(out=o[:], in_=s[:], func=ACT.Relu)
+                    nc.sync.dma_start(out=out[rt * 128:(rt + 1) * 128, h * 512:(h + 1) * 512], in_=o[:])

@@ -43,10 +43,7 @@ def tile_extremeoptimizationlayer_pa_kernel(tc, x, W, b, gamma, beta, Wf1_bytes,
             r = wpool.tile([P, 4, D_OUT], BF16, name="wraw", bufs=4, align_bytes=64)
             wraw[i, kg] = r
             v = W[i, kg * 512:(kg + 1) * 512, :].rearrange("(p j) n -> p j n", j=4)
-            if i == 0 and kg == 0:
-                nc.sync.dma_start(out=r[:, :, 0:512], in_=v[:, :, 0:512])
-            else:
-                nc.sync.dma_start(out=r[:], in_=v)
+            nc.sync.dma_start(out=r[:], in_=v)
 
         def load_f(i, g):
             s = 2 * i + g
@@ -55,8 +52,6 @@ def tile_extremeoptimizationlayer_pa_kernel(tc, x, W, b, gamma, beta, Wf1_bytes,
             nc.sync.dma_start(out=r[:], in_=Wf1_bytes[s * 512:(s + 1) * 512, :].rearrange("(p t) n -> p t n", t=4))
 
         def pe_interleave(i, kg, blk):
-            if blk == 0:
-                wgrp_of(i, kg)
             n0 = D_OUT - 256 * (N_PI[kg] - blk)
             bank = pip.tile([P, 4, 64, 4], BF16, name="pi", tag="pi")
             pib[i, kg, blk] = bank
@@ -67,6 +62,7 @@ def tile_extremeoptimizationlayer_pa_kernel(tc, x, W, b, gamma, beta, Wf1_bytes,
 
         def pe_exit(i, kg, blk):
             m0 = 256 - 64 * (N_PI[kg] - blk)
+            wgrp_of(i, kg)
             nc.scalar.copy(out=wgrp[i, kg][:, :, m0:m0 + 64, :].rearrange("p t m j -> p t (m j)"),
                            in_=pib[i, kg, blk][:].rearrange("p t m j -> p t (m j)"))
 
@@ -106,46 +102,35 @@ def tile_extremeoptimizationlayer_pa_kernel(tc, x, W, b, gamma, beta, Wf1_bytes,
 
         def relu(i, bk):
             g, th = divmod(bk, 2)
+            if bk == 0:
+                sm(i, "sum")
             if th == 0:
                 a = hpool.tile([P, 4, ROWS], F32, name="act", bufs=4, align_bytes=64)
                 act[i, g] = a
             for u in range(2):
                 t = 2 * th + u
                 nc.scalar.activation(out=act[i, g][:, t, :], in_=s1b[i, bk][:, u, :], func=ACT.Relu,
-                                     bias=prm[:, t, 2 * i + g:2 * i + g + 1])
+                                     bias=prm[:, t, 2 * i + g:2 * i + g + 1], accum_out=small[i, "sum"][:, t, g:g + 1])
 
-        def bn(i, g):
-            if g == 0:
-                st = hpool.tile([P, 4, 2, 6], F32, name="st", bufs=2)
-                stats[i] = st
+        def neg_mean(i):
+            nm = sm(i, "nm")
+            nc.scalar.activation(out=nm[:], in_=small[i, "sum"][:], func=ACT.Copy, scale=-1.0 / ROWS)
+            sm(i, "ssq")
+
+        def square(i, g):
             for t in range(4):
-                nc.vector.bn_stats(out=stats[i][:, t, g, :], in_=act[i, g][:, t, :])
+                junk = hpool.tile([P, ROWS], BF16, name="junk", bufs=2)
+                nc.scalar.activation(out=junk[:], in_=act[i, g][:, t, :], func=ACT.Square,
+                                     bias=small[i, "nm"][:, t, g:g + 1], accum_out=small[i, "ssq"][:, t, g:g + 1])
 
         def sm(i, name, shape=(4, 2)):
             tl = hpool.tile([P] + list(shape), F32, name="sm_" + name, bufs=2)
             small[i, name] = tl
             return tl
 
-        def st_sums(i):
-            st = stats[i]
-            sv = sm(i, "sv", (4, 2, 2))
-            nc.vector.tensor_tensor(out=sv[:], in0=st[:, :, :, 1:3], in1=st[:, :, :, 4:6], op=ALU.add)
-            dm = sm(i, "dm")
-            nc.vector.tensor_tensor(out=dm[:], in0=st[:, :, :, 1], in1=st[:, :, :, 4], op=ALU.subtract)
-
-        def st_d2(i):
-            d2 = sm(i, "d2")
-            dm = small[i, "dm"]
-            nc.vector.scalar_tensor_tensor(out=d2[:], in0=dm[:], scalar=0.25, in1=dm[:], op0=ALU.mult, op1=ALU.mult)
-
-        def st_var(i):
-            var = sm(i, "var")
-            nc.vector.scalar_tensor_tensor(out=var[:], in0=small[i, "sv"][:, :, :, 1], scalar=1.0 / 256, in1=small[i, "d2"][:],
-                                           op0=ALU.mult, op1=ALU.add)
-
         def st_sqrt(i):
             sd = sm(i, "sd")
-            nc.scalar.activation(out=sd[:], in_=small[i, "var"][:], func=ACT.Sqrt, bias=EPS)
+            nc.scalar.activation(out=sd[:], in_=small[i, "ssq"][:], func=ACT.Sqrt, scale=1.0 / ROWS, bias=EPS)
 
         def st_recip(i):
             rs = sm(i, "rs")
@@ -157,19 +142,22 @@ def tile_extremeoptimizationlayer_pa_kernel(tc, x, W, b, gamma, beta, Wf1_bytes,
 
         def st_ms(i):
             ms = sm(i, "ms")
-            nc.vector.scalar_tensor_tensor(out=ms[:], in0=small[i, "sv"][:, :, :, 0], scalar=-0.5, in1=small[i, "sc"][:],
-                                           op0=ALU.mult, op1=ALU.mult)
+            nc.vector.tensor_tensor(out=ms[:], in0=small[i, "nm"][:], in1=small[i, "sc"][:], op=ALU.mult)
 
         def st_shift(i):
             sh = sm(i, "sh")
             nc.vector.tensor_tensor(out=sh[:], in0=small[i, "ms"][:], in1=prm[:, :, 32 + 2 * i:34 + 2 * i], op=ALU.add)
 
-        def norm(i, g):
+        def norm(i, g, eng):
             n = hpool.tile([P, 4, ROWS], BF16, name="nrm", bufs=3, align_bytes=64)
             nrm[i, g] = n
             for t in range(4):
-                nc.scalar.activation(out=n[:, t, :], in_=act[i, g][:, t, :], func=ACT.Identity,
-                                     scale=small[i, "sc"][:, t, g:g + 1], bias=small[i, "sh"][:, t, g:g + 1])
+                scale, shift = small[i, "sc"][:, t, g:g + 1], small[i, "sh"][:, t, g:g + 1]
+                if eng is nc.vector:
+                    eng.tensor_scalar(out=n[:, t, :], in0=act[i, g][:, t, :], scalar1=scale, scalar2=shift,
+                                      op0=ALU.mult, op1=ALU.add)
+                else:
+                    eng.activation(out=n[:, t, :], in_=act[i, g][:, t, :], func=ACT.Identity, scale=scale, bias=shift)
 
         def u_interleave(i, g):
             u = hpool.tile([P, 4 * ROWS], BF16, name="ugrp", bufs=3, align_bytes=64)
@@ -183,14 +171,18 @@ def tile_extremeoptimizationlayer_pa_kernel(tc, x, W, b, gamma, beta, Wf1_bytes,
             ucod[i, g], uscl[i, g] = c, s
             nc.vector.quantize_mx(out=c[:].bitcast(FP8X4), scales=s[:], in_=ugrp[i, g][:])
 
-        def f_widen(i, g, ts):
-            if ts[0] == 0:
+        def f_widen(i, g, ts, vts=(3,)):
+            if (i, g) not in fwid:
                 w = fpool.tile([P, 4, D_OUT], BF16, name="fwid", bufs=3, align_bytes=64)
                 fwid[i, g] = w
             s = 2 * i + g
             for t in ts:
-                nc.scalar.activation(out=fwid[i, g][:, t, :], in_=fraw[i, g][:, t, :].bitcast(FP8), func=ACT.Copy,
-                                     scale=scl[:, t, s:s + 1])
+                if t in vts:
+                    nc.vector.tensor_scalar(out=fwid[i, g][:, t, :], in0=fraw[i, g][:, t, :].bitcast(FP8),
+                                            scalar1=scl[:, t, s:s + 1], scalar2=None, op0=ALU.mult)
+                else:
+                    nc.scalar.activation(out=fwid[i, g][:, t, :], in_=fraw[i, g][:, t, :].bitcast(FP8), func=ACT.Copy,
+                                         scale=scl[:, t, s:s + 1])
 
         def f_interleave(i, g, h):
             if h == 0:
@@ -202,8 +194,8 @@ def tile_extremeoptimizationlayer_pa_kernel(tc, x, W, b, gamma, beta, Wf1_bytes,
 
         def f_quant(i, g, h):
             if h == 0:
-                c = fpool.tile([P, D_OUT], U32, name="fcod", bufs=3, align_bytes=64)
-                s = fpool.tile([P, D_OUT], U8, name="fscl", bufs=3, align_bytes=64)
+                c = fpool.tile([P, D_OUT], U32, name="fcod", bufs=4, align_bytes=64)
+                s = fpool.tile([P, D_OUT], U8, name="fscl", bufs=4, align_bytes=64)
                 fcod[i, g], fscl[i, g] = c, s
             cols = slice(h * 512, (h + 1) * 512)
             nc.vector.quantize_mx(out=fcod[i, g][:, cols].bitcast(FP8X4), scales=fscl[i, g][:, cols],
@@ -230,21 +222,19 @@ def tile_extremeoptimizationlayer_pa_kernel(tc, x, W, b, gamma, beta, Wf1_bytes,
         nc.vector.memset(dummy[:], 1.0)
         make_identity(nc, ident_f[:])
         make_identity(nc, ident_b[:])
-        xs = []
+        nc.scalar.dma_start(out=srow[0:16, :], in_=Wf1_scale.rearrange("(s c) o -> s (o c)", c=512))
+        load_f(0, 0)
+        nc.scalar.dma_start(out=prow[0:16, :], in_=b.rearrange("k (g c) -> (k g) c", c=512))
+        nc.scalar.dma_start(out=prow[16:32, :], in_=gamma.rearrange("k (g c) -> (k g) c", c=512))
+        nc.scalar.dma_start(out=prow[32:48, :], in_=beta.rearrange("k (g c) -> (k g) c", c=512))
         load_w(0, 0)
+        xs = []
         for rt in range(2):
             xt = keep.tile([P, D_IN], BF16, name="xs" + str(rt), align_bytes=64)
             xs.append(xt)
             nc.sync.dma_start(out=xt[:], in_=x[rt * 128:(rt + 1) * 128, :])
-        nc.sync.dma_start(out=wraw[0, 0][:, :, 512:1024],
-                          in_=W[0, 0:512, 512:1024].rearrange("(p j) n -> p j n", j=4))
-        load_f(0, 0)
         load_w(0, 1)
         load_f(0, 1)
-        nc.scalar.dma_start(out=srow[0:16, :], in_=Wf1_scale.rearrange("(s c) o -> s (o c)", c=512))
-        nc.scalar.dma_start(out=prow[0:16, :], in_=b.rearrange("k (g c) -> (k g) c", c=512))
-        nc.scalar.dma_start(out=prow[16:32, :], in_=gamma.rearrange("k (g c) -> (k g) c", c=512))
-        nc.scalar.dma_start(out=prow[32:48, :], in_=beta.rearrange("k (g c) -> (k g) c", c=512))
         nc.scalar.activation(out=dummy2[:], in_=dummy[:], func=ACT.Sqrt)
 
         scl = keep.tile([P, 4, 16], F32, name="scl")
@@ -264,6 +254,17 @@ def tile_extremeoptimizationlayer_pa_kernel(tc, x, W, b, gamma, beta, Wf1_bytes,
             for t in range(4):
                 nc.tensor.transpose(ps[:, t, :], srow[:, t:512:4], ident_f[:])
             nc.scalar.copy(out=scl[:], in_=ps[:, :, 0:16])
+            f_widen(0, 0, (0, 2, 1, 3), (2, 3))
+            f_interleave(0, 0, 0)
+            f_interleave(0, 0, 1)
+            f_quant(0, 0, 0)
+            f_quant(0, 0, 1)
+            pp = pip.tile([P, 4, 128], BF16, name="pp", tag="pi")
+            for t in range(4):
+                nc.tensor.transpose(pp[:, t, :], prow[:, t:512:4], ident_b[:])
+            nc.scalar.copy(out=prm[:], in_=pp[:, :, 0:48])
+            pe_interleave(0, 0, 0)
+            pe_interleave(0, 0, 1)
             for kg in range(2):
                 xp = s1p.tile([P, 2, ROWS], F32, name="xp", tag="s1")
                 for rt in range(2):
@@ -272,10 +273,6 @@ def tile_extremeoptimizationlayer_pa_kernel(tc, x, W, b, gamma, beta, Wf1_bytes,
                                             xs[rt][:].bitcast(F32)[:, 256 * kg + u:256 * (kg + 1):2], ident_f[:])
                 nc.scalar.copy(out=xgrp[:, kg, :].bitcast(F32).rearrange("p (r u) -> p r u", u=2),
                                in_=xp[:].rearrange("p u r -> p r u"))
-            pp = pip.tile([P, 4, 128], BF16, name="pp", tag="pi")
-            for t in range(4):
-                nc.tensor.transpose(pp[:, t, :], prow[:, t:512:4], ident_b[:])
-            nc.scalar.copy(out=prm[:], in_=pp[:, :, 0:48])
 
             for i in range(-1, BRANCHES):
                 cur, nxt = i >= 0, i + 1 < BRANCHES
@@ -290,66 +287,71 @@ def tile_extremeoptimizationlayer_pa_kernel(tc, x, W, b, gamma, beta, Wf1_bytes,
                     mm1(i, 0)
                     mm1(i, 1)
                 if nxt:
-                    pe_interleave(i + 1, 0, 0)
-                    pe_interleave(i + 1, 0, 1)
                     w_interleave(i + 1, 0)
                 if cur:
                     relu(i, 0)
-                    relu(i, 1)
                     mm1(i, 2)
+                    relu(i, 1)
                     mm1(i, 3)
+                    if i > 0:
+                        mm2(i - 1, 0)
+                        mm2(i - 1, 1)
                     relu(i, 2)
                     relu(i, 3)
-                    bn(i, 0)
+                    f_interleave(i, 1, 0)
                 if nxt:
                     pe_exit(i + 1, 0, 0)
                     pe_exit(i + 1, 0, 1)
                     pe_interleave(i + 1, 1, 0)
                 if cur:
-                    bn(i, 1)
-                    if i > 0:
-                        mm2(i - 1, 1)
+                    neg_mean(i)
+                    f_interleave(i, 1, 1)
+                    square(i, 0)
+                    square(i, 1)
                 if i == -1:
                     nc.vector.quantize_mx(out=xcod[:].bitcast(FP8X4), scales=xscl[:],
                                           in_=xgrp[:].rearrange("p k c -> p (k c)"))
                 if nxt:
                     w_quant(i + 1, 0)
-                if cur:
-                    st_sums(i)
-                if nxt:
                     w_interleave(i + 1, 1)
                 if cur:
-                    f_widen(i, 1, (0, 1, 2, 3))
-                    st_d2(i)
-                    f_interleave(i, 0, 0)
-                    st_var(i)
-                    f_interleave(i, 0, 1)
+                    if nxt:
+                        f_widen(i + 1, 0, (0,))
                     st_sqrt(i)
+                    if nxt:
+                        f_widen(i + 1, 0, (3, 1, 2))
                 if nxt:
                     pe_exit(i + 1, 1, 0)
-                    f_widen(i + 1, 0, (0, 1, 2))
+                if i + 2 < BRANCHES:
+                    pe_interleave(i + 2, 0, 0)
+                    pe_interleave(i + 2, 0, 1)
                 if cur:
                     st_recip(i)
-                    f_quant(i, 0, 0)
+                    f_quant(i, 1, 0)
                     st_scale(i)
-                    f_quant(i, 0, 1)
+                    f_quant(i, 1, 1)
                     st_ms(i)
-                    f_interleave(i, 1, 0)
+                if nxt and cur:
+                    f_widen(i + 1, 1, (3,))
+                if cur:
                     st_shift(i)
-                    f_interleave(i, 1, 1)
-                    norm(i, 0)
-                    norm(i, 1)
+                    norm(i, 0, nc.scalar)
+                    norm(i, 1, nc.scalar if nxt else nc.vector)
+                    if nxt:
+                        f_interleave(i + 1, 0, 0)
+                        f_interleave(i + 1, 0, 1)
                 if nxt:
-                    f_widen(i + 1, 0, (3,))
+                    f_widen(i + 1, 1, (0, 1, 2) if cur else (0, 1, 2, 3), (3,) if cur else ())
                     w_quant(i + 1, 1)
                 if cur:
                     u_interleave(i, 0)
                     u_interleave(i, 1)
                     u_quant(i, 0)
-                    mm2(i, 0)
                     u_quant(i, 1)
-                    f_quant(i, 1, 0)
-                    f_quant(i, 1, 1)
+                    if nxt:
+                        f_quant(i + 1, 0, 0)
+                        f_quant(i + 1, 0, 1)
+            mm2(BRANCHES - 1, 0)
             mm2(BRANCHES - 1, 1)
 
             for h in range(2):

@@ -18,7 +18,11 @@ ALU = mybir.AluOpType
 ENG = mybir.EngineType
 
 P = 128
-N_PI = (2, 1)
+V_WIDEN = ([(2, 3), (2, 3)] + [(2, 3), (3,)]) * 4
+
+
+def n_pi(i, kg):
+    return ((0, 0), (1, 1), (2, 2), (2, 2), (2, 2), (2, 2), (2, 2), (2, 1))[i][kg]
 
 
 def tile_extremeoptimizationlayer_pa_kernel(tc, x, W, b, gamma, beta, Wf1_bytes, Wf1_scale, bf1, out):
@@ -52,39 +56,43 @@ def tile_extremeoptimizationlayer_pa_kernel(tc, x, W, b, gamma, beta, Wf1_bytes,
             nc.sync.dma_start(out=r[:], in_=Wf1_bytes[s * 512:(s + 1) * 512, :].rearrange("(p t) n -> p t n", t=4))
 
         def pe_interleave(i, kg, blk):
-            n0 = D_OUT - 256 * (N_PI[kg] - blk)
-            bank = pip.tile([P, 4, 64, 4], BF16, name="pi", tag="pi")
+            g, t0 = pe_block(i, kg, blk)
+            bank = pip.tile([P, 2, 128, 4], BF16, name="pi", tag="pi")
             pib[i, kg, blk] = bank
-            v = wraw[i, kg][:, :, n0:n0 + 256].rearrange("p j (m t) -> p t m j", t=4)
-            for th in range(2):
-                nc.tensor.matmul(out=bank[:, 2 * th:2 * th + 2, :, :].rearrange("p t m j -> p (t m j)"), lhsT=ident_b[:],
-                                 rhs=v[:, 2 * th:2 * th + 2], start=True, stop=True)
+            v = wraw[i, kg][:, :, g * 512:(g + 1) * 512].rearrange("p j (m t) -> p t m j", t=4)
+            for u in range(2):
+                nc.tensor.matmul(out=bank[:, u, :, :].rearrange("p m j -> p (m j)"), lhsT=ident_b[:],
+                                 rhs=v[:, t0 + u], start=True, stop=True)
 
-        def pe_exit(i, kg, blk):
-            m0 = 256 - 64 * (N_PI[kg] - blk)
-            wgrp_of(i, kg)
-            nc.scalar.copy(out=wgrp[i, kg][:, :, m0:m0 + 64, :].rearrange("p t m j -> p t (m j)"),
-                           in_=pib[i, kg, blk][:].rearrange("p t m j -> p t (m j)"))
+        def pe_block(i, kg, blk):
+            return divmod(8 - 2 * (n_pi(i, kg) - blk), 4)
 
         def wgrp_of(i, kg):
             if (i, kg) not in wgrp:
-                wg = wpool.tile([P, 4, 256, 4], BF16, name="wgrp", bufs=3, align_bytes=64)
+                wg = wpool.tile([P, 2, 4, 128, 4], BF16, name="wgrp", bufs=3, align_bytes=64)
                 wgrp[i, kg] = wg
             return wgrp[i, kg]
 
+        def pe_exit(i, kg, blk):
+            g, t0 = pe_block(i, kg, blk)
+            nc.scalar.copy(out=wgrp_of(i, kg)[:, g, t0:t0 + 2, :, :].rearrange("p t m j -> p (t m j)"),
+                           in_=pib[i, kg, blk][:].rearrange("p t m j -> p (t m j)"))
+
         def w_interleave(i, kg):
-            n1 = D_OUT - 256 * N_PI[kg]
-            g = wgrp_of(i, kg)
-            nc.vector.tensor_copy(
-                out=g[:, :, 0:n1 // 4, :].rearrange("p t (c m) j -> p c t m j", m=2),
-                in_=wraw[i, kg][:, :, 0:n1].rearrange("p j (c m t) -> p c t m j", m=2, t=4))
+            for g in range(2):
+                nt = min(4, 8 - 2 * n_pi(i, kg) - 4 * g)
+                if nt > 0:
+                    nc.vector.tensor_copy(
+                        out=wgrp_of(i, kg)[:, g, 0:nt, :, :].rearrange("p t (c m) j -> p c t j m", m=2),
+                        in_=wraw[i, kg][:, :, g * 512:(g + 1) * 512].rearrange(
+                            "p j (c m t) -> p c t j m", m=2, t=4)[:, :, 0:nt])
 
         def w_quant(i, kg):
             c = wpool.tile([P, D_OUT], U32, name="wcod", bufs=4, align_bytes=64)
             s = wpool.tile([P, D_OUT], U8, name="wscl", bufs=4, align_bytes=64)
             wcod[i, kg], wscl[i, kg] = c, s
             nc.vector.quantize_mx(out=c[:].bitcast(FP8X4), scales=s[:],
-                                  in_=wgrp[i, kg][:].rearrange("p t m j -> p (t m j)"))
+                                  in_=wgrp[i, kg][:].rearrange("p g t m j -> p (g t m j)"))
 
         def mm1(i, bk):
             g, th = divmod(bk, 2)
@@ -92,7 +100,7 @@ def tile_extremeoptimizationlayer_pa_kernel(tc, x, W, b, gamma, beta, Wf1_bytes,
             s1b[i, bk] = bank
             for u in range(2):
                 t = 2 * th + u
-                cols = slice(t * 256 + g * 128, t * 256 + g * 128 + 128)
+                cols = slice((g * 4 + t) * 128, (g * 4 + t + 1) * 128)
                 for kg in range(2):
                     nc.tensor.matmul_mx(out=bank[:, u, :],
                                         lhsT=wcod[i, kg][:, cols].bitcast(FP8X4), lhsT_scale=wscl[i, kg][:, cols],
@@ -149,31 +157,37 @@ def tile_extremeoptimizationlayer_pa_kernel(tc, x, W, b, gamma, beta, Wf1_bytes,
             nc.vector.tensor_tensor(out=sh[:], in0=small[i, "ms"][:], in1=prm[:, :, 32 + 2 * i:34 + 2 * i], op=ALU.add)
 
         def norm(i, g, eng):
-            n = hpool.tile([P, 4, ROWS], BF16, name="nrm", bufs=3, align_bytes=64)
-            nrm[i, g] = n
+            if g == 0:
+                n = hpool.tile([P, 4, 2 * ROWS], BF16, name="nrm", bufs=2, align_bytes=64)
+                nrm[i] = n
             for t in range(4):
                 scale, shift = small[i, "sc"][:, t, g:g + 1], small[i, "sh"][:, t, g:g + 1]
+                o = nrm[i][:, t, g * ROWS:(g + 1) * ROWS]
                 if eng is nc.vector:
-                    eng.tensor_scalar(out=n[:, t, :], in0=act[i, g][:, t, :], scalar1=scale, scalar2=shift,
+                    eng.tensor_scalar(out=o, in0=act[i, g][:, t, :], scalar1=scale, scalar2=shift,
                                       op0=ALU.mult, op1=ALU.add)
                 else:
-                    eng.activation(out=n[:, t, :], in_=act[i, g][:, t, :], func=ACT.Identity, scale=scale, bias=shift)
+                    eng.activation(out=o, in_=act[i, g][:, t, :], func=ACT.Identity, scale=scale, bias=shift)
 
-        def u_interleave(i, g):
-            u = hpool.tile([P, 4 * ROWS], BF16, name="ugrp", bufs=3, align_bytes=64)
-            ugrp[i, g] = u
-            nc.vector.tensor_copy(out=u[:].rearrange("p (c i t) -> p c t i", i=4, t=4),
-                                  in_=nrm[i, g][:].rearrange("p t (c i) -> p c t i", i=4))
+        def u_interleave(i, g0, g1):
+            if i not in ugrp:
+                u = hpool.tile([P, 2 * ROWS * 4], BF16, name="ugrp", bufs=2, align_bytes=64)
+                ugrp[i] = u
+            nc.vector.tensor_copy(
+                out=ugrp[i][:, g0 * 4 * ROWS:g1 * 4 * ROWS].rearrange("p (c i t) -> p c t i", i=4, t=4),
+                in_=nrm[i][:, :, g0 * ROWS:g1 * ROWS].rearrange("p t (c i) -> p c t i", i=4))
 
-        def u_quant(i, g):
-            c = hpool.tile([P, ROWS], U32, name="ucod", bufs=3, align_bytes=64)
-            s = hpool.tile([P, ROWS], U8, name="uscl", bufs=3, align_bytes=64)
-            ucod[i, g], uscl[i, g] = c, s
-            nc.vector.quantize_mx(out=c[:].bitcast(FP8X4), scales=s[:], in_=ugrp[i, g][:])
+        def u_quant(i, g0, g1):
+            if i not in ucod:
+                c = hpool.tile([P, 2 * ROWS], U32, name="ucod", bufs=2, align_bytes=64)
+                s = hpool.tile([P, 2 * ROWS], U8, name="uscl", bufs=2, align_bytes=64)
+                ucod[i], uscl[i] = c, s
+            nc.vector.quantize_mx(out=ucod[i][:, g0 * ROWS:g1 * ROWS].bitcast(FP8X4), scales=uscl[i][:, g0 * ROWS:g1 * ROWS],
+                                  in_=ugrp[i][:, g0 * 4 * ROWS:g1 * 4 * ROWS])
 
         def f_widen(i, g, ts, vts=(3,)):
             if (i, g) not in fwid:
-                w = fpool.tile([P, 4, D_OUT], BF16, name="fwid", bufs=3, align_bytes=64)
+                w = fpool.tile([P, 4, D_OUT], BF16, name="fwid", bufs=4, align_bytes=64)
                 fwid[i, g] = w
             s = 2 * i + g
             for t in ts:
@@ -184,32 +198,33 @@ def tile_extremeoptimizationlayer_pa_kernel(tc, x, W, b, gamma, beta, Wf1_bytes,
                     nc.scalar.activation(out=fwid[i, g][:, t, :], in_=fraw[i, g][:, t, :].bitcast(FP8), func=ACT.Copy,
                                          scale=scl[:, t, s:s + 1])
 
-        def f_interleave(i, g, h):
-            if h == 0:
+        def f_interleave(i, g, c0=0, c1=D_OUT):
+            if c0 == 0:
                 f = fpool.tile([P, 4 * D_OUT], BF16, name="fgrp", bufs=2, align_bytes=64)
                 fgrp[i, g] = f
             nc.vector.tensor_copy(
-                out=fgrp[i, g][:, h * 2048:(h + 1) * 2048].rearrange("p (c i t) -> p c t i", i=4, t=4),
-                in_=fwid[i, g][:, :, h * 512:(h + 1) * 512].rearrange("p t (c i) -> p c t i", i=4))
+                out=fgrp[i, g][:, 4 * c0:4 * c1].rearrange("p (c i t) -> p c t i", i=4, t=4),
+                in_=fwid[i, g][:, :, c0:c1].rearrange("p t (c i) -> p c t i", i=4))
 
-        def f_quant(i, g, h):
-            if h == 0:
+        def f_quant(i, g, c0=0, c1=D_OUT):
+            if c0 == 0:
                 c = fpool.tile([P, D_OUT], U32, name="fcod", bufs=4, align_bytes=64)
                 s = fpool.tile([P, D_OUT], U8, name="fscl", bufs=4, align_bytes=64)
                 fcod[i, g], fscl[i, g] = c, s
-            cols = slice(h * 512, (h + 1) * 512)
-            nc.vector.quantize_mx(out=fcod[i, g][:, cols].bitcast(FP8X4), scales=fscl[i, g][:, cols],
-                                  in_=fgrp[i, g][:, h * 2048:(h + 1) * 2048])
+            nc.vector.quantize_mx(out=fcod[i, g][:, c0:c1].bitcast(FP8X4), scales=fscl[i, g][:, c0:c1],
+                                  in_=fgrp[i, g][:, 4 * c0:4 * c1])
+
+        def mm2_pass(i, g, h, rt, last=False):
+            rows, cols = slice(g * ROWS + rt * 128, g * ROWS + (rt + 1) * 128), slice(h * 512, (h + 1) * 512)
+            nc.tensor.matmul_mx(out=acc[h, rt][:],
+                                lhsT=ucod[i][:, rows].bitcast(FP8X4), lhsT_scale=uscl[i][:, rows],
+                                rhs=fcod[i, g][:, cols].bitcast(FP8X4), rhs_scale=fscl[i, g][:, cols],
+                                start=(i == 0 and g == 0), stop=last)
 
         def mm2(i, g):
-            first, last = (i == 0 and g == 0), (i == BRANCHES - 1 and g == 1)
             for h in range(2):
                 for rt in range(2):
-                    rows, cols = slice(rt * 128, (rt + 1) * 128), slice(h * 512, (h + 1) * 512)
-                    nc.tensor.matmul_mx(out=acc[h, rt][:],
-                                        lhsT=ucod[i, g][:, rows].bitcast(FP8X4), lhsT_scale=uscl[i, g][:, rows],
-                                        rhs=fcod[i, g][:, cols].bitcast(FP8X4), rhs_scale=fscl[i, g][:, cols],
-                                        start=first, stop=last)
+                    mm2_pass(i, g, h, rt)
 
         prow = keep.tile([P, 512], BF16, name="prow", align_bytes=64)
         srow = keep.tile([P, 512], F32, name="srow", align_bytes=64)
@@ -228,13 +243,13 @@ def tile_extremeoptimizationlayer_pa_kernel(tc, x, W, b, gamma, beta, Wf1_bytes,
         nc.scalar.dma_start(out=prow[16:32, :], in_=gamma.rearrange("k (g c) -> (k g) c", c=512))
         nc.scalar.dma_start(out=prow[32:48, :], in_=beta.rearrange("k (g c) -> (k g) c", c=512))
         load_w(0, 0)
+        load_f(0, 1)
         xs = []
         for rt in range(2):
             xt = keep.tile([P, D_IN], BF16, name="xs" + str(rt), align_bytes=64)
             xs.append(xt)
             nc.sync.dma_start(out=xt[:], in_=x[rt * 128:(rt + 1) * 128, :])
         load_w(0, 1)
-        load_f(0, 1)
         nc.scalar.activation(out=dummy2[:], in_=dummy[:], func=ACT.Sqrt)
 
         scl = keep.tile([P, 4, 16], F32, name="scl")
@@ -255,16 +270,7 @@ def tile_extremeoptimizationlayer_pa_kernel(tc, x, W, b, gamma, beta, Wf1_bytes,
                 nc.tensor.transpose(ps[:, t, :], srow[:, t:512:4], ident_f[:])
             nc.scalar.copy(out=scl[:], in_=ps[:, :, 0:16])
             f_widen(0, 0, (0, 2, 1, 3), (2, 3))
-            f_interleave(0, 0, 0)
-            f_interleave(0, 0, 1)
-            f_quant(0, 0, 0)
-            f_quant(0, 0, 1)
-            pp = pip.tile([P, 4, 128], BF16, name="pp", tag="pi")
-            for t in range(4):
-                nc.tensor.transpose(pp[:, t, :], prow[:, t:512:4], ident_b[:])
-            nc.scalar.copy(out=prm[:], in_=pp[:, :, 0:48])
-            pe_interleave(0, 0, 0)
-            pe_interleave(0, 0, 1)
+            f_widen(0, 1, (0, 1))
             for kg in range(2):
                 xp = s1p.tile([P, 2, ROWS], F32, name="xp", tag="s1")
                 for rt in range(2):
@@ -274,6 +280,11 @@ def tile_extremeoptimizationlayer_pa_kernel(tc, x, W, b, gamma, beta, Wf1_bytes,
                 nc.scalar.copy(out=xgrp[:, kg, :].bitcast(F32).rearrange("p (r u) -> p r u", u=2),
                                in_=xp[:].rearrange("p u r -> p r u"))
 
+            f_widen(0, 1, (2, 3), ())
+            pp = pip.tile([P, 4, 128], BF16, name="pp", tag="pi")
+            for t in range(4):
+                nc.tensor.transpose(pp[:, t, :], prow[:, t:512:4], ident_b[:])
+            nc.scalar.copy(out=prm[:], in_=pp[:, :, 0:48])
             for i in range(-1, BRANCHES):
                 cur, nxt = i >= 0, i + 1 < BRANCHES
                 if i + 2 < BRANCHES:
@@ -283,76 +294,87 @@ def tile_extremeoptimizationlayer_pa_kernel(tc, x, W, b, gamma, beta, Wf1_bytes,
                     load_f(i + 2, 1)
                 if i == 1:
                     nc.sync.dma_start(out=bf1b[:], in_=bf1.partition_broadcast(128))
+                nx2 = i + 2 < BRANCHES
+                nx2 = i + 2 < BRANCHES
+                nx2 = i + 2 < BRANCHES
+                nx2 = i + 2 < BRANCHES
+                nx2 = i + 2 < BRANCHES
+                nx2 = i + 2 < BRANCHES
                 if cur:
                     mm1(i, 0)
                     mm1(i, 1)
                 if nxt:
                     w_interleave(i + 1, 0)
+                    for k in range(n_pi(i + 1, 0)):
+                        pe_exit(i + 1, 0, k)
                 if cur:
                     relu(i, 0)
                     mm1(i, 2)
                     relu(i, 1)
                     mm1(i, 3)
-                    if i > 0:
-                        mm2(i - 1, 0)
-                        mm2(i - 1, 1)
                     relu(i, 2)
                     relu(i, 3)
-                    f_interleave(i, 1, 0)
+                    f_interleave(i, 0)
                 if nxt:
-                    pe_exit(i + 1, 0, 0)
-                    pe_exit(i + 1, 0, 1)
-                    pe_interleave(i + 1, 1, 0)
+                    for k in range(n_pi(i + 1, 1)):
+                        pe_interleave(i + 1, 1, k)
+                if i > 0:
+                    mm2(i - 1, 0)
+                    mm2(i - 1, 1)
                 if cur:
                     neg_mean(i)
-                    f_interleave(i, 1, 1)
                     square(i, 0)
                     square(i, 1)
+                    st_sqrt(i)
+                if nxt:
+                    for k in range(n_pi(i + 1, 1)):
+                        pe_exit(i + 1, 1, k)
+                    w_quant(i + 1, 0)
+                    w_interleave(i + 1, 1)
                 if i == -1:
                     nc.vector.quantize_mx(out=xcod[:].bitcast(FP8X4), scales=xscl[:],
                                           in_=xgrp[:].rearrange("p k c -> p (k c)"))
-                if nxt:
-                    w_quant(i + 1, 0)
-                    w_interleave(i + 1, 1)
                 if cur:
-                    if nxt:
-                        f_widen(i + 1, 0, (0,))
-                    st_sqrt(i)
-                    if nxt:
-                        f_widen(i + 1, 0, (3, 1, 2))
-                if nxt:
-                    pe_exit(i + 1, 1, 0)
-                if i + 2 < BRANCHES:
-                    pe_interleave(i + 2, 0, 0)
-                    pe_interleave(i + 2, 0, 1)
-                if cur:
+                    if not nxt:
+                        f_interleave(i, 1)
+                    f_quant(i, 0)
                     st_recip(i)
-                    f_quant(i, 1, 0)
+                    if nxt:
+                        f_widen(i + 1, 0, (3, 0, 1))
+                    else:
+                        f_quant(i, 1, 0, 512)
                     st_scale(i)
-                    f_quant(i, 1, 1)
+                    if nxt:
+                        f_widen(i + 1, 0, (2,), V_WIDEN[2 * i + 2])
+                    else:
+                        f_quant(i, 1, 512, 1024)
                     st_ms(i)
-                if nxt and cur:
-                    f_widen(i + 1, 1, (3,))
-                if cur:
+                    if nxt:
+                        f_widen(i + 1, 1, V_WIDEN[2 * i + 3], V_WIDEN[2 * i + 3])
                     st_shift(i)
+                if nx2:
+                    for k in range(n_pi(i + 2, 0)):
+                        pe_interleave(i + 2, 0, k)
+                if cur:
                     norm(i, 0, nc.scalar)
                     norm(i, 1, nc.scalar if nxt else nc.vector)
-                    if nxt:
-                        f_interleave(i + 1, 0, 0)
-                        f_interleave(i + 1, 0, 1)
                 if nxt:
-                    f_widen(i + 1, 1, (0, 1, 2) if cur else (0, 1, 2, 3), (3,) if cur else ())
                     w_quant(i + 1, 1)
                 if cur:
-                    u_interleave(i, 0)
-                    u_interleave(i, 1)
-                    u_quant(i, 0)
-                    u_quant(i, 1)
                     if nxt:
-                        f_quant(i + 1, 0, 0)
-                        f_quant(i + 1, 0, 1)
-            mm2(BRANCHES - 1, 0)
-            mm2(BRANCHES - 1, 1)
+                        f_widen(i + 1, 1, [t for t in range(4) if t not in V_WIDEN[2 * i + 3]], ())
+                        f_interleave(i, 1)
+                        u_interleave(i, 0, 2)
+                        f_quant(i, 1)
+                        u_quant(i, 0, 2)
+                    else:
+                        u_interleave(i, 1, 2)
+                        u_interleave(i, 0, 1)
+                        u_quant(i, 1, 2)
+                        u_quant(i, 0, 1)
+            for bank in ((0, 0), (0, 1), (1, 0), (1, 1)):
+                mm2_pass(BRANCHES - 1, 1, *bank)
+                mm2_pass(BRANCHES - 1, 0, *bank, last=True)
 
             for h in range(2):
                 for rt in range(2):

@@ -18,11 +18,18 @@ ALU = mybir.AluOpType
 ENG = mybir.EngineType
 
 P = 128
-V_WIDEN = ([(2, 3), (2, 3)] + [(2, 3), (3,)]) * 4
+SLOTS = 4
+K_PASS = P * SLOTS
+PASSES_1 = D_IN // K_PASS
+BANK = 512
+
+OTHER_BLOCKS = ((1, 1), (1, 1), (2, 2), (2, 2), (2, 2), (2, 2), (2, 2), (2, 1))
 
 
-def n_pi(i, kg):
-    return ((0, 0), (1, 1), (2, 2), (2, 2), (2, 2), (2, 2), (2, 2), (2, 1))[i][kg]
+def vector_slots(i, half):
+    if i == 0:
+        return (2, 3) if half == 0 else ()
+    return (3,) if half == 1 and i % 2 == 1 else (2, 3)
 
 
 def tile_extremeoptimizationlayer_pa_kernel(tc, x, W, b, gamma, beta, Wf1_bytes, Wf1_scale, bf1, out):
@@ -33,353 +40,357 @@ def tile_extremeoptimizationlayer_pa_kernel(tc, x, W, b, gamma, beta, Wf1_bytes,
         fpool = ctx.enter_context(tc.tile_pool(name="fpool", bufs=1))
         hpool = ctx.enter_context(tc.tile_pool(name="hpool", bufs=1))
         opool = ctx.enter_context(tc.tile_pool(name="opool", bufs=4))
-        accp = ctx.enter_context(tc.psum_pool(name="accp", bufs=1))
-        s1p = ctx.enter_context(tc.psum_pool(name="s1p", bufs=2))
-        pip = ctx.enter_context(tc.psum_pool(name="pip", bufs=2))
+        acc_pool = ctx.enter_context(tc.psum_pool(name="acc_pool", bufs=1))
+        ps1_pool = ctx.enter_context(tc.psum_pool(name="ps1_pool", bufs=2))
+        inter_pool = ctx.enter_context(tc.psum_pool(name="inter_pool", bufs=2))
 
-        wraw, wgrp, wcod, wscl = {}, {}, {}, {}
-        fraw, fwid, fgrp, fcod, fscl = {}, {}, {}, {}, {}
-        act, nrm, ugrp, ucod, uscl = {}, {}, {}, {}, {}
-        pib, s1b = {}, {}
-        stats, small = {}, {}
+        w_raw, w_mix, w_codes, w_scales, w_bank = {}, {}, {}, {}, {}
+        f_bytes, f_wide, f_mix, f_codes, f_scales = {}, {}, {}, {}, {}
+        act, act_bank, normed, u_mix, u_codes, u_scales = {}, {}, {}, {}, {}, {}
+        stat = {}
 
-        def load_w(i, kg):
-            r = wpool.tile([P, 4, D_OUT], BF16, name="wraw", bufs=4, align_bytes=64)
-            wraw[i, kg] = r
-            v = W[i, kg * 512:(kg + 1) * 512, :].rearrange("(p j) n -> p j n", j=4)
-            nc.sync.dma_start(out=r[:], in_=v)
 
-        def load_f(i, g):
-            s = 2 * i + g
-            r = fpool.tile([P, 4, D_OUT], U8, name="fraw", bufs=5, align_bytes=64)
-            fraw[i, g] = r
-            nc.sync.dma_start(out=r[:], in_=Wf1_bytes[s * 512:(s + 1) * 512, :].rearrange("(p t) n -> p t n", t=4))
+        def load_w(i, kp):
+            w_raw[i, kp] = wpool.tile([P, SLOTS, D_OUT], BF16, name="w_raw", bufs=4, align_bytes=64)
+            rows = W[i, kp * K_PASS:(kp + 1) * K_PASS, :]
+            nc.sync.dma_start(out=w_raw[i, kp][:], in_=rows.rearrange("(p t) n -> p t n", t=SLOTS))
 
-        def pe_interleave(i, kg, blk):
-            g, t0 = pe_block(i, kg, blk)
-            bank = pip.tile([P, 2, 128, 4], BF16, name="pi", tag="pi")
-            pib[i, kg, blk] = bank
-            v = wraw[i, kg][:, :, g * 512:(g + 1) * 512].rearrange("p j (m t) -> p t m j", t=4)
-            for u in range(2):
-                nc.tensor.matmul(out=bank[:, u, :, :].rearrange("p m j -> p (m j)"), lhsT=ident_b[:],
-                                 rhs=v[:, t0 + u], start=True, stop=True)
+        def load_f(i, half):
+            row0 = i * D_OUT + half * K_PASS
+            f_bytes[i, half] = fpool.tile([P, SLOTS, D_OUT], U8, name="f_bytes", bufs=5, align_bytes=64)
+            nc.sync.dma_start(out=f_bytes[i, half][:],
+                              in_=Wf1_bytes[row0:row0 + K_PASS, :].rearrange("(p t) n -> p t n", t=SLOTS))
 
-        def pe_block(i, kg, blk):
-            return divmod(8 - 2 * (n_pi(i, kg) - blk), 4)
 
-        def wgrp_of(i, kg):
-            if (i, kg) not in wgrp:
-                wg = wpool.tile([P, 2, 4, 128, 4], BF16, name="wgrp", bufs=3, align_bytes=64)
-                wgrp[i, kg] = wg
-            return wgrp[i, kg]
+        def w_mix_of(i, kp):
+            if (i, kp) not in w_mix:
+                w_mix[i, kp] = wpool.tile([P, 2, SLOTS, P, SLOTS], BF16, name="w_mix", bufs=3, align_bytes=64)
+            return w_mix[i, kp]
 
-        def pe_exit(i, kg, blk):
-            g, t0 = pe_block(i, kg, blk)
-            nc.scalar.copy(out=wgrp_of(i, kg)[:, g, t0:t0 + 2, :, :].rearrange("p t m j -> p (t m j)"),
-                           in_=pib[i, kg, blk][:].rearrange("p t m j -> p (t m j)"))
+        def w_half(i, kp, half):
+            return w_raw[i, kp][:, :, half * K_PASS:(half + 1) * K_PASS]
 
-        def w_interleave(i, kg):
-            for g in range(2):
-                nt = min(4, 8 - 2 * n_pi(i, kg) - 4 * g)
-                if nt > 0:
+        def w_interleave(i, kp):
+            tiles = 2 * (4 - OTHER_BLOCKS[i][kp])
+            for half in range(2):
+                slots = min(SLOTS, tiles - SLOTS * half)
+                if slots > 0:
                     nc.vector.tensor_copy(
-                        out=wgrp_of(i, kg)[:, g, 0:nt, :, :].rearrange("p t (c m) j -> p c t j m", m=2),
-                        in_=wraw[i, kg][:, :, g * 512:(g + 1) * 512].rearrange(
-                            "p j (c m t) -> p c t j m", m=2, t=4)[:, :, 0:nt])
+                        out=w_mix_of(i, kp)[:, half, 0:slots].rearrange("p q (c m) t -> p c q m t", m=2),
+                        in_=w_half(i, kp, half).rearrange("p t (c m q) -> p c q m t", m=2, q=SLOTS)[:, :, 0:slots])
 
-        def w_quant(i, kg):
-            c = wpool.tile([P, D_OUT], U32, name="wcod", bufs=4, align_bytes=64)
-            s = wpool.tile([P, D_OUT], U8, name="wscl", bufs=4, align_bytes=64)
-            wcod[i, kg], wscl[i, kg] = c, s
-            nc.vector.quantize_mx(out=c[:].bitcast(FP8X4), scales=s[:],
-                                  in_=wgrp[i, kg][:].rearrange("p g t m j -> p (g t m j)"))
+        def scalar_interleave(i, kp):
+            for s in (2, 3):
+                nc.scalar.copy(out=w_mix_of(i, kp)[:, 1, s],
+                               in_=w_half(i, kp, 1).rearrange("p t (m q) -> p q m t", q=SLOTS)[:, s])
 
-        def mm1(i, bk):
-            g, th = divmod(bk, 2)
-            bank = s1p.tile([P, 2, ROWS], F32, name="s1", tag="s1")
-            s1b[i, bk] = bank
+        def block_place(i, kp, blk):
+            return divmod(2 * (4 - OTHER_BLOCKS[i][kp] + blk), SLOTS)
+
+        def tensor_interleave(i, kp, blk):
+            half, s0 = block_place(i, kp, blk)
+            bank = inter_pool.tile([P, 2, P, SLOTS], BF16, name="inter_bank", tag="inter")
+            w_bank[i, kp, blk] = bank
+            moving = w_half(i, kp, half).rearrange("p t (m q) -> p q m t", q=SLOTS)
             for u in range(2):
-                t = 2 * th + u
-                cols = slice((g * 4 + t) * 128, (g * 4 + t + 1) * 128)
-                for kg in range(2):
+                nc.tensor.matmul(out=bank[:, u].rearrange("p m t -> p (m t)"), lhsT=ident_b[:],
+                                 rhs=moving[:, s0 + u], start=True, stop=True)
+
+        def tensor_block_out(i, kp, blk):
+            half, s0 = block_place(i, kp, blk)
+            nc.scalar.copy(out=w_mix_of(i, kp)[:, half, s0:s0 + 2].rearrange("p s m t -> p (s m t)"),
+                           in_=w_bank[i, kp, blk][:].rearrange("p s m t -> p (s m t)"))
+
+        def tensor_blocks(i, kp):
+            return range(OTHER_BLOCKS[i][kp] if i > 0 else 0)
+
+        def w_quant(i, kp):
+            w_codes[i, kp] = wpool.tile([P, D_OUT], U32, name="w_codes", bufs=4, align_bytes=64)
+            w_scales[i, kp] = wpool.tile([P, D_OUT], U8, name="w_scales", bufs=4, align_bytes=64)
+            nc.vector.quantize_mx(out=w_codes[i, kp][:].bitcast(FP8X4), scales=w_scales[i, kp][:],
+                                  in_=w_mix[i, kp][:].rearrange("p h s m t -> p (h s m t)"))
+
+
+        def f_widen(i, half, slots):
+            if (i, half) not in f_wide:
+                f_wide[i, half] = fpool.tile([P, SLOTS, D_OUT], BF16, name="f_wide", bufs=4, align_bytes=64)
+            for t in slots:
+                wide, byte = f_wide[i, half][:, t, :], f_bytes[i, half][:, t, :].bitcast(FP8)
+                scale = f_row_scale[:, t, 2 * i + half:2 * i + half + 1]
+                if t in vector_slots(i, half):
+                    nc.vector.tensor_scalar(out=wide, in0=byte, scalar1=scale, scalar2=None, op0=ALU.mult)
+                else:
+                    nc.scalar.activation(out=wide, in_=byte, func=ACT.Copy, scale=scale)
+
+        def f_interleave(i, half, c0=0, c1=D_OUT):
+            if c0 == 0:
+                f_mix[i, half] = fpool.tile([P, SLOTS * D_OUT], BF16, name="f_mix", bufs=2, align_bytes=64)
+            nc.vector.tensor_copy(
+                out=f_mix[i, half][:, SLOTS * c0:SLOTS * c1].rearrange("p (c m t) -> p c t m", m=4, t=SLOTS),
+                in_=f_wide[i, half][:, :, c0:c1].rearrange("p t (c m) -> p c t m", m=4))
+
+        def f_quant(i, half, c0=0, c1=D_OUT):
+            if c0 == 0:
+                f_codes[i, half] = fpool.tile([P, D_OUT], U32, name="f_codes", bufs=4, align_bytes=64)
+                f_scales[i, half] = fpool.tile([P, D_OUT], U8, name="f_scales", bufs=4, align_bytes=64)
+            nc.vector.quantize_mx(out=f_codes[i, half][:, c0:c1].bitcast(FP8X4), scales=f_scales[i, half][:, c0:c1],
+                                  in_=f_mix[i, half][:, SLOTS * c0:SLOTS * c1])
+
+
+        def stage1(i, pair):
+            half, s0 = divmod(2 * pair, SLOTS)
+            bank = ps1_pool.tile([P, 2, ROWS], F32, name="act_bank", tag="ps1")
+            act_bank[i, pair] = bank
+            for u in range(2):
+                col0 = (half * SLOTS + s0 + u) * P
+                cols = slice(col0, col0 + P)
+                for kp in range(PASSES_1):
+                    rows = slice(kp * ROWS, (kp + 1) * ROWS)
                     nc.tensor.matmul_mx(out=bank[:, u, :],
-                                        lhsT=wcod[i, kg][:, cols].bitcast(FP8X4), lhsT_scale=wscl[i, kg][:, cols],
-                                        rhs=xcod[:, kg * 256:(kg + 1) * 256].bitcast(FP8X4),
-                                        rhs_scale=xscl[:, kg * 256:(kg + 1) * 256],
-                                        start=(kg == 0), stop=(kg == 1))
+                                        lhsT=w_codes[i, kp][:, cols].bitcast(FP8X4), lhsT_scale=w_scales[i, kp][:, cols],
+                                        rhs=x_codes[:, rows].bitcast(FP8X4), rhs_scale=x_scales[:, rows],
+                                        start=(kp == 0), stop=(kp == PASSES_1 - 1))
 
-        def relu(i, bk):
-            g, th = divmod(bk, 2)
-            if bk == 0:
-                sm(i, "sum")
-            if th == 0:
-                a = hpool.tile([P, 4, ROWS], F32, name="act", bufs=4, align_bytes=64)
-                act[i, g] = a
-            for u in range(2):
-                t = 2 * th + u
-                nc.scalar.activation(out=act[i, g][:, t, :], in_=s1b[i, bk][:, u, :], func=ACT.Relu,
-                                     bias=prm[:, t, 2 * i + g:2 * i + g + 1], accum_out=small[i, "sum"][:, t, g:g + 1])
+        def stat_tile(i, name):
+            stat[i, name] = hpool.tile([P, SLOTS, 2], F32, name="stat_" + name, bufs=2)
+            return stat[i, name]
+
+        def relu(i, pair):
+            half, s0 = divmod(2 * pair, SLOTS)
+            if pair == 0:
+                stat_tile(i, "sum")
+            if s0 == 0:
+                act[i, half] = hpool.tile([P, SLOTS, ROWS], F32, name="act", bufs=4, align_bytes=64)
+            for s in (s0, s0 + 1):
+                nc.scalar.activation(out=act[i, half][:, s, :], in_=act_bank[i, pair][:, s - s0, :], func=ACT.Relu,
+                                     bias=params[:, s, 2 * i + half:2 * i + half + 1],
+                                     accum_out=stat[i, "sum"][:, s, half:half + 1])
 
         def neg_mean(i):
-            nm = sm(i, "nm")
-            nc.scalar.activation(out=nm[:], in_=small[i, "sum"][:], func=ACT.Copy, scale=-1.0 / ROWS)
-            sm(i, "ssq")
+            nc.scalar.activation(out=stat_tile(i, "neg_mean")[:], in_=stat[i, "sum"][:], func=ACT.Copy, scale=-1.0 / ROWS)
 
-        def square(i, g):
-            for t in range(4):
-                junk = hpool.tile([P, ROWS], BF16, name="junk", bufs=2)
-                nc.scalar.activation(out=junk[:], in_=act[i, g][:, t, :], func=ACT.Square,
-                                     bias=small[i, "nm"][:, t, g:g + 1], accum_out=small[i, "ssq"][:, t, g:g + 1])
+        def squares(i):
+            sums = stat_tile(i, "squares")
+            for half in range(2):
+                for s in range(SLOTS):
+                    square = hpool.tile([P, ROWS], BF16, name="square", bufs=2)
+                    nc.scalar.activation(out=square[:], in_=act[i, half][:, s, :], func=ACT.Square,
+                                         bias=stat[i, "neg_mean"][:, s, half:half + 1], accum_out=sums[:, s, half:half + 1])
 
-        def sm(i, name, shape=(4, 2)):
-            tl = hpool.tile([P] + list(shape), F32, name="sm_" + name, bufs=2)
-            small[i, name] = tl
-            return tl
+        def std(i):
+            nc.scalar.activation(out=stat_tile(i, "std")[:], in_=stat[i, "squares"][:], func=ACT.Sqrt,
+                                 scale=1.0 / ROWS, bias=EPS)
 
-        def st_sqrt(i):
-            sd = sm(i, "sd")
-            nc.scalar.activation(out=sd[:], in_=small[i, "ssq"][:], func=ACT.Sqrt, scale=1.0 / ROWS, bias=EPS)
+        def inv_std(i):
+            nc.vector.reciprocal(out=stat_tile(i, "inv_std")[:], in_=stat[i, "std"][:])
 
-        def st_recip(i):
-            rs = sm(i, "rs")
-            nc.vector.reciprocal(out=rs[:], in_=small[i, "sd"][:])
+        def norm_scale(i):
+            nc.vector.tensor_tensor(out=stat_tile(i, "scale")[:], in0=stat[i, "inv_std"][:],
+                                    in1=params[:, :, 16 + 2 * i:18 + 2 * i], op=ALU.mult)
 
-        def st_scale(i):
-            sc = sm(i, "sc")
-            nc.vector.tensor_tensor(out=sc[:], in0=small[i, "rs"][:], in1=prm[:, :, 16 + 2 * i:18 + 2 * i], op=ALU.mult)
+        def norm_offset(i):
+            nc.vector.tensor_tensor(out=stat_tile(i, "offset")[:], in0=stat[i, "neg_mean"][:], in1=stat[i, "scale"][:],
+                                    op=ALU.mult)
 
-        def st_ms(i):
-            ms = sm(i, "ms")
-            nc.vector.tensor_tensor(out=ms[:], in0=small[i, "nm"][:], in1=small[i, "sc"][:], op=ALU.mult)
+        def norm_shift(i):
+            nc.vector.tensor_tensor(out=stat_tile(i, "shift")[:], in0=stat[i, "offset"][:],
+                                    in1=params[:, :, 32 + 2 * i:34 + 2 * i], op=ALU.add)
 
-        def st_shift(i):
-            sh = sm(i, "sh")
-            nc.vector.tensor_tensor(out=sh[:], in0=small[i, "ms"][:], in1=prm[:, :, 32 + 2 * i:34 + 2 * i], op=ALU.add)
 
-        def norm(i, g, eng):
-            if g == 0:
-                n = hpool.tile([P, 4, 2 * ROWS], BF16, name="nrm", bufs=2, align_bytes=64)
-                nrm[i] = n
-            for t in range(4):
-                scale, shift = small[i, "sc"][:, t, g:g + 1], small[i, "sh"][:, t, g:g + 1]
-                o = nrm[i][:, t, g * ROWS:(g + 1) * ROWS]
-                if eng is nc.vector:
-                    eng.tensor_scalar(out=o, in0=act[i, g][:, t, :], scalar1=scale, scalar2=shift,
-                                      op0=ALU.mult, op1=ALU.add)
+        def normalise(i, half, engine):
+            if half == 0:
+                normed[i] = hpool.tile([P, SLOTS, 2 * ROWS], BF16, name="normed", bufs=2, align_bytes=64)
+            for s in range(SLOTS):
+                result, a = normed[i][:, s, half * ROWS:(half + 1) * ROWS], act[i, half][:, s, :]
+                scale, shift = stat[i, "scale"][:, s, half:half + 1], stat[i, "shift"][:, s, half:half + 1]
+                if engine is nc.vector:
+                    engine.tensor_scalar(out=result, in0=a, scalar1=scale, scalar2=shift, op0=ALU.mult, op1=ALU.add)
                 else:
-                    eng.activation(out=o, in_=act[i, g][:, t, :], func=ACT.Identity, scale=scale, bias=shift)
+                    engine.activation(out=result, in_=a, func=ACT.Identity, scale=scale, bias=shift)
 
-        def u_interleave(i, g0, g1):
-            if i not in ugrp:
-                u = hpool.tile([P, 2 * ROWS * 4], BF16, name="ugrp", bufs=2, align_bytes=64)
-                ugrp[i] = u
+        def u_interleave(i, half0, half1):
+            if i not in u_mix:
+                u_mix[i] = hpool.tile([P, 2 * ROWS * SLOTS], BF16, name="u_mix", bufs=2, align_bytes=64)
+            r0, r1 = half0 * ROWS, half1 * ROWS
             nc.vector.tensor_copy(
-                out=ugrp[i][:, g0 * 4 * ROWS:g1 * 4 * ROWS].rearrange("p (c i t) -> p c t i", i=4, t=4),
-                in_=nrm[i][:, :, g0 * ROWS:g1 * ROWS].rearrange("p t (c i) -> p c t i", i=4))
+                out=u_mix[i][:, SLOTS * r0:SLOTS * r1].rearrange("p (c m t) -> p c t m", m=4, t=SLOTS),
+                in_=normed[i][:, :, r0:r1].rearrange("p t (c m) -> p c t m", m=4))
 
-        def u_quant(i, g0, g1):
-            if i not in ucod:
-                c = hpool.tile([P, 2 * ROWS], U32, name="ucod", bufs=2, align_bytes=64)
-                s = hpool.tile([P, 2 * ROWS], U8, name="uscl", bufs=2, align_bytes=64)
-                ucod[i], uscl[i] = c, s
-            nc.vector.quantize_mx(out=ucod[i][:, g0 * ROWS:g1 * ROWS].bitcast(FP8X4), scales=uscl[i][:, g0 * ROWS:g1 * ROWS],
-                                  in_=ugrp[i][:, g0 * 4 * ROWS:g1 * 4 * ROWS])
+        def u_quant(i, half0, half1):
+            if i not in u_codes:
+                u_codes[i] = hpool.tile([P, 2 * ROWS], U32, name="u_codes", bufs=2, align_bytes=64)
+                u_scales[i] = hpool.tile([P, 2 * ROWS], U8, name="u_scales", bufs=2, align_bytes=64)
+            r0, r1 = half0 * ROWS, half1 * ROWS
+            nc.vector.quantize_mx(out=u_codes[i][:, r0:r1].bitcast(FP8X4), scales=u_scales[i][:, r0:r1],
+                                  in_=u_mix[i][:, SLOTS * r0:SLOTS * r1])
 
-        def f_widen(i, g, ts, vts=(3,)):
-            if (i, g) not in fwid:
-                w = fpool.tile([P, 4, D_OUT], BF16, name="fwid", bufs=4, align_bytes=64)
-                fwid[i, g] = w
-            s = 2 * i + g
-            for t in ts:
-                if t in vts:
-                    nc.vector.tensor_scalar(out=fwid[i, g][:, t, :], in0=fraw[i, g][:, t, :].bitcast(FP8),
-                                            scalar1=scl[:, t, s:s + 1], scalar2=None, op0=ALU.mult)
-                else:
-                    nc.scalar.activation(out=fwid[i, g][:, t, :], in_=fraw[i, g][:, t, :].bitcast(FP8), func=ACT.Copy,
-                                         scale=scl[:, t, s:s + 1])
 
-        def f_interleave(i, g, c0=0, c1=D_OUT):
-            if c0 == 0:
-                f = fpool.tile([P, 4 * D_OUT], BF16, name="fgrp", bufs=2, align_bytes=64)
-                fgrp[i, g] = f
-            nc.vector.tensor_copy(
-                out=fgrp[i, g][:, 4 * c0:4 * c1].rearrange("p (c i t) -> p c t i", i=4, t=4),
-                in_=fwid[i, g][:, :, c0:c1].rearrange("p t (c i) -> p c t i", i=4))
+        def stage2(i, half, n_half, row_tile, stop=False):
+            rows = slice(half * ROWS + row_tile * P, half * ROWS + (row_tile + 1) * P)
+            cols = slice(n_half * BANK, (n_half + 1) * BANK)
+            nc.tensor.matmul_mx(out=acc[n_half, row_tile][:],
+                                lhsT=u_codes[i][:, rows].bitcast(FP8X4), lhsT_scale=u_scales[i][:, rows],
+                                rhs=f_codes[i, half][:, cols].bitcast(FP8X4), rhs_scale=f_scales[i, half][:, cols],
+                                start=(i == 0 and half == 0), stop=stop)
 
-        def f_quant(i, g, c0=0, c1=D_OUT):
-            if c0 == 0:
-                c = fpool.tile([P, D_OUT], U32, name="fcod", bufs=4, align_bytes=64)
-                s = fpool.tile([P, D_OUT], U8, name="fscl", bufs=4, align_bytes=64)
-                fcod[i, g], fscl[i, g] = c, s
-            nc.vector.quantize_mx(out=fcod[i, g][:, c0:c1].bitcast(FP8X4), scales=fscl[i, g][:, c0:c1],
-                                  in_=fgrp[i, g][:, 4 * c0:4 * c1])
 
-        def mm2_pass(i, g, h, rt, last=False):
-            rows, cols = slice(g * ROWS + rt * 128, g * ROWS + (rt + 1) * 128), slice(h * 512, (h + 1) * 512)
-            nc.tensor.matmul_mx(out=acc[h, rt][:],
-                                lhsT=ucod[i][:, rows].bitcast(FP8X4), lhsT_scale=uscl[i][:, rows],
-                                rhs=fcod[i, g][:, cols].bitcast(FP8X4), rhs_scale=fscl[i, g][:, cols],
-                                start=(i == 0 and g == 0), stop=last)
-
-        def mm2(i, g):
-            for h in range(2):
-                for rt in range(2):
-                    mm2_pass(i, g, h, rt)
-
-        prow = keep.tile([P, 512], BF16, name="prow", align_bytes=64)
-        srow = keep.tile([P, 512], F32, name="srow", align_bytes=64)
+        param_rows = keep.tile([P, K_PASS], BF16, name="param_rows", align_bytes=64)
+        scale_rows = keep.tile([P, K_PASS], F32, name="scale_rows", align_bytes=64)
         ident_f = keep.tile([P, P], F32, name="ident_f", align_bytes=64)
         ident_b = keep.tile([P, P], BF16, name="ident_b", align_bytes=64)
-        dummy = keep.tile([P, 1], F32, name="dummy")
-        dummy2 = keep.tile([P, 1], F32, name="dummy2")
-        nc.vector.memset(srow[:], 0.0)
-        nc.vector.memset(prow[:], 0.0)
-        nc.vector.memset(dummy[:], 1.0)
+        one = keep.tile([P, 1], F32, name="one")
+        warm = keep.tile([P, 1], F32, name="warm")
+        f_row_scale = keep.tile([P, SLOTS, 16], F32, name="f_row_scale")
+        params = keep.tile([P, SLOTS, 48], F32, name="params")
+        x_rows = keep.tile([P, 2, D_IN], BF16, name="x_rows", align_bytes=64)
+        x_mix = keep.tile([P, PASSES_1, ROWS * SLOTS], BF16, name="x_mix", align_bytes=64)
+        x_codes = keep.tile([P, PASSES_1 * ROWS], U32, name="x_codes", align_bytes=64)
+        x_scales = keep.tile([P, PASSES_1 * ROWS], U8, name="x_scales", align_bytes=64)
+        bf1_all = keep.tile([P, D_OUT], BF16, name="bf1_all", align_bytes=64)
+        acc = {}
+        for n_half in range(2):
+            for row_tile in range(2):
+                acc[n_half, row_tile] = acc_pool.tile([P, BANK], F32, name="acc" + str(2 * n_half + row_tile))
+
+        nc.vector.memset(scale_rows[:], 0.0)
+        nc.vector.memset(param_rows[:], 0.0)
+        nc.vector.memset(one[:], 1.0)
         make_identity(nc, ident_f[:])
         make_identity(nc, ident_b[:])
-        nc.scalar.dma_start(out=srow[0:16, :], in_=Wf1_scale.rearrange("(s c) o -> s (o c)", c=512))
+        nc.scalar.dma_start(out=scale_rows[0:16, :], in_=Wf1_scale.rearrange("(s c) o -> s (o c)", c=K_PASS))
         load_f(0, 0)
-        nc.scalar.dma_start(out=prow[0:16, :], in_=b.rearrange("k (g c) -> (k g) c", c=512))
-        nc.scalar.dma_start(out=prow[16:32, :], in_=gamma.rearrange("k (g c) -> (k g) c", c=512))
-        nc.scalar.dma_start(out=prow[32:48, :], in_=beta.rearrange("k (g c) -> (k g) c", c=512))
+        for n, vector in enumerate((b, gamma, beta)):
+            nc.scalar.dma_start(out=param_rows[16 * n:16 * (n + 1), :], in_=vector.rearrange("k (h c) -> (k h) c", c=K_PASS))
         load_w(0, 0)
         load_f(0, 1)
-        xs = []
-        for rt in range(2):
-            xt = keep.tile([P, D_IN], BF16, name="xs" + str(rt), align_bytes=64)
-            xs.append(xt)
-            nc.sync.dma_start(out=xt[:], in_=x[rt * 128:(rt + 1) * 128, :])
+        for row_tile in range(2):
+            nc.sync.dma_start(out=x_rows[:, row_tile, :], in_=x[row_tile * P:(row_tile + 1) * P, :])
         load_w(0, 1)
-        nc.scalar.activation(out=dummy2[:], in_=dummy[:], func=ACT.Sqrt)
-
-        scl = keep.tile([P, 4, 16], F32, name="scl")
-        prm = keep.tile([P, 4, 48], F32, name="prm")
-        xgrp = keep.tile([P, 2, 1024], BF16, name="xgrp", align_bytes=64)
-        xcod = keep.tile([P, 512], U32, name="xcod", align_bytes=64)
-        xscl = keep.tile([P, 512], U8, name="xscl", align_bytes=64)
-        bf1b = keep.tile([P, D_OUT], BF16, name="bf1b", align_bytes=64)
-        acc = {}
-        for h in range(2):
-            for rt in range(2):
-                a = accp.tile([P, 512], F32, name="acc" + str(2 * h + rt))
-                acc[h, rt] = a
+        nc.scalar.activation(out=warm[:], in_=one[:], func=ACT.Sqrt)
 
         with tc.manual_schedule(engines={ENG.PE, ENG.Activation, ENG.DVE, ENG.SP}):
-            ps = s1p.tile([P, 4, 128], F32, name="ps", tag="s1")
-            for t in range(4):
-                nc.tensor.transpose(ps[:, t, :], srow[:, t:512:4], ident_f[:])
-            nc.scalar.copy(out=scl[:], in_=ps[:, :, 0:16])
-            f_widen(0, 0, (0, 2, 1, 3), (2, 3))
+            bank = ps1_pool.tile([P, SLOTS, P], F32, name="scale_bank", tag="ps1")
+            for t in range(SLOTS):
+                nc.tensor.transpose(bank[:, t, :], scale_rows[:, t:K_PASS:SLOTS], ident_f[:])
+            nc.scalar.copy(out=f_row_scale[:], in_=bank[:, :, 0:16])
+            f_widen(0, 0, range(SLOTS))
+            scalar_interleave(0, 0)
             f_widen(0, 1, (0, 1))
-            for kg in range(2):
-                xp = s1p.tile([P, 2, ROWS], F32, name="xp", tag="s1")
-                for rt in range(2):
-                    for u in range(2):
-                        nc.tensor.transpose(xp[:, u, rt * 128:(rt + 1) * 128],
-                                            xs[rt][:].bitcast(F32)[:, 256 * kg + u:256 * (kg + 1):2], ident_f[:])
-                nc.scalar.copy(out=xgrp[:, kg, :].bitcast(F32).rearrange("p (r u) -> p r u", u=2),
-                               in_=xp[:].rearrange("p u r -> p r u"))
 
-            f_widen(0, 1, (2, 3), ())
-            pp = pip.tile([P, 4, 128], BF16, name="pp", tag="pi")
-            for t in range(4):
-                nc.tensor.transpose(pp[:, t, :], prow[:, t:512:4], ident_b[:])
-            nc.scalar.copy(out=prm[:], in_=pp[:, :, 0:48])
+            for kp in range(PASSES_1):
+                bank = ps1_pool.tile([P, 2, ROWS], F32, name="x_bank", tag="ps1")
+                words = slice(kp * K_PASS // 2, (kp + 1) * K_PASS // 2)
+                for row_tile in range(2):
+                    for u in range(2):
+                        nc.tensor.transpose(bank[:, u, row_tile * P:(row_tile + 1) * P],
+                                            x_rows[:, row_tile, :].bitcast(F32)[:, words][:, u::2], ident_f[:])
+                nc.scalar.copy(out=x_mix[:, kp, :].bitcast(F32).rearrange("p (r u) -> p r u", u=2),
+                               in_=bank[:].rearrange("p u r -> p r u"))
+
+            scalar_interleave(0, 1)
+            f_widen(0, 1, (2, 3))
+            bank = inter_pool.tile([P, SLOTS, P], BF16, name="param_bank", tag="inter")
+            for s in range(SLOTS):
+                nc.tensor.transpose(bank[:, s, :], param_rows[:, s:K_PASS:SLOTS], ident_b[:])
+            nc.scalar.copy(out=params[:], in_=bank[:, :, 0:48])
+
             for i in range(-1, BRANCHES):
-                cur, nxt = i >= 0, i + 1 < BRANCHES
-                if i + 2 < BRANCHES:
-                    load_w(i + 2, 0)
-                    load_f(i + 2, 0)
-                    load_w(i + 2, 1)
-                    load_f(i + 2, 1)
+                cur, nxt, nxt2 = i >= 0, i + 1 < BRANCHES, i + 2 < BRANCHES
+                if nxt2:
+                    for half in range(2):
+                        load_w(i + 2, half)
+                        load_f(i + 2, half)
                 if i == 1:
-                    nc.sync.dma_start(out=bf1b[:], in_=bf1.partition_broadcast(128))
-                nx2 = i + 2 < BRANCHES
-                nx2 = i + 2 < BRANCHES
-                nx2 = i + 2 < BRANCHES
-                nx2 = i + 2 < BRANCHES
-                nx2 = i + 2 < BRANCHES
-                nx2 = i + 2 < BRANCHES
+                    nc.sync.dma_start(out=bf1_all[:], in_=bf1.partition_broadcast(P))
+
                 if cur:
-                    mm1(i, 0)
-                    mm1(i, 1)
+                    stage1(i, 0)
+                    stage1(i, 1)
                 if nxt:
                     w_interleave(i + 1, 0)
-                    for k in range(n_pi(i + 1, 0)):
-                        pe_exit(i + 1, 0, k)
+                for pair in range(4):
+                    if cur:
+                        if pair >= 2:
+                            stage1(i, pair)
+                        relu(i, pair)
+                    if nxt and pair in tensor_blocks(i + 1, 0):
+                        tensor_block_out(i + 1, 0, pair)
                 if cur:
-                    relu(i, 0)
-                    mm1(i, 2)
-                    relu(i, 1)
-                    mm1(i, 3)
-                    relu(i, 2)
-                    relu(i, 3)
-                    f_interleave(i, 0)
+                    f_interleave(i, 0, BANK if i == 0 else 0)
                 if nxt:
-                    for k in range(n_pi(i + 1, 1)):
-                        pe_interleave(i + 1, 1, k)
+                    for blk in tensor_blocks(i + 1, 1):
+                        tensor_interleave(i + 1, 1, blk)
                 if i > 0:
-                    mm2(i - 1, 0)
-                    mm2(i - 1, 1)
+                    for half in range(2):
+                        for n_half in range(2):
+                            for row_tile in range(2):
+                                stage2(i - 1, half, n_half, row_tile)
                 if cur:
                     neg_mean(i)
-                    square(i, 0)
-                    square(i, 1)
-                    st_sqrt(i)
+                    squares(i)
+                    std(i)
                 if nxt:
-                    for k in range(n_pi(i + 1, 1)):
-                        pe_exit(i + 1, 1, k)
+                    for blk in tensor_blocks(i + 1, 1):
+                        tensor_block_out(i + 1, 1, blk)
                     w_quant(i + 1, 0)
+                    if not cur:
+                        f_interleave(0, 0, 0, BANK)
                     w_interleave(i + 1, 1)
-                if i == -1:
-                    nc.vector.quantize_mx(out=xcod[:].bitcast(FP8X4), scales=xscl[:],
-                                          in_=xgrp[:].rearrange("p k c -> p (k c)"))
-                if cur:
-                    if not nxt:
-                        f_interleave(i, 1)
-                    f_quant(i, 0)
-                    st_recip(i)
-                    if nxt:
-                        f_widen(i + 1, 0, (3, 0, 1))
-                    else:
-                        f_quant(i, 1, 0, 512)
-                    st_scale(i)
-                    if nxt:
-                        f_widen(i + 1, 0, (2,), V_WIDEN[2 * i + 2])
-                    else:
-                        f_quant(i, 1, 512, 1024)
-                    st_ms(i)
-                    if nxt:
-                        f_widen(i + 1, 1, V_WIDEN[2 * i + 3], V_WIDEN[2 * i + 3])
-                    st_shift(i)
-                if nx2:
-                    for k in range(n_pi(i + 2, 0)):
-                        pe_interleave(i + 2, 0, k)
-                if cur:
-                    norm(i, 0, nc.scalar)
-                    norm(i, 1, nc.scalar if nxt else nc.vector)
-                if nxt:
-                    w_quant(i + 1, 1)
-                if cur:
-                    if nxt:
-                        f_widen(i + 1, 1, [t for t in range(4) if t not in V_WIDEN[2 * i + 3]], ())
-                        f_interleave(i, 1)
-                        u_interleave(i, 0, 2)
-                        f_quant(i, 1)
-                        u_quant(i, 0, 2)
-                    else:
-                        u_interleave(i, 1, 2)
-                        u_interleave(i, 0, 1)
-                        u_quant(i, 1, 2)
-                        u_quant(i, 0, 1)
-            for bank in ((0, 0), (0, 1), (1, 0), (1, 1)):
-                mm2_pass(BRANCHES - 1, 1, *bank)
-                mm2_pass(BRANCHES - 1, 0, *bank, last=True)
+                if not cur:
+                    nc.vector.quantize_mx(out=x_codes[:].bitcast(FP8X4), scales=x_scales[:],
+                                          in_=x_mix[:].rearrange("p k c -> p (k c)"))
 
-            for h in range(2):
-                for rt in range(2):
-                    s = opool.tile([P, 512], F32, name="osum", align_bytes=64)
-                    o = opool.tile([P, 512], F32, name="ores", align_bytes=64)
-                    nc.vector.tensor_tensor(out=s[:], in0=acc[h, rt][:], in1=bf1b[:, h * 512:(h + 1) * 512], op=ALU.add)
-                    nc.scalar.activation(out=o[:], in_=s[:], func=ACT.Relu)
-                    nc.sync.dma_start(out=out[rt * 128:(rt + 1) * 128, h * 512:(h + 1) * 512], in_=o[:])
+                if cur and nxt:
+                    f_quant(i, 0)
+                    inv_std(i)
+                    f_widen(i + 1, 0, (3, 0, 1))
+                    norm_scale(i)
+                    f_widen(i + 1, 0, (2,))
+                    norm_offset(i)
+                    f_widen(i + 1, 1, vector_slots(i + 1, 1))
+                    norm_shift(i)
+                elif cur:
+                    f_interleave(i, 1)
+                    f_quant(i, 0)
+                    inv_std(i)
+                    f_quant(i, 1, 0, BANK)
+                    norm_scale(i)
+                    f_quant(i, 1, BANK, D_OUT)
+                    norm_offset(i)
+                    norm_shift(i)
+                if nxt2:
+                    for blk in tensor_blocks(i + 2, 0):
+                        tensor_interleave(i + 2, 0, blk)
+                if cur and nxt:
+                    normalise(i, 0, nc.scalar)
+                    normalise(i, 1, nc.scalar)
+                    w_quant(i + 1, 1)
+                    f_widen(i + 1, 1, [t for t in range(SLOTS) if t not in vector_slots(i + 1, 1)])
+                    f_interleave(i, 1)
+                    u_interleave(i, 0, 2)
+                    f_quant(i, 1)
+                    u_quant(i, 0, 2)
+                elif cur:
+                    normalise(i, 0, nc.scalar)
+                    normalise(i, 1, nc.vector)
+                    u_interleave(i, 1, 2)
+                    u_interleave(i, 0, 1)
+                    u_quant(i, 1, 2)
+                    u_quant(i, 0, 1)
+                else:
+                    w_quant(0, 1)
+
+            banks = [(n_half, row_tile) for n_half in range(2) for row_tile in range(2)]
+            for n_half, row_tile in banks:
+                stage2(BRANCHES - 1, 1, n_half, row_tile)
+                stage2(BRANCHES - 1, 0, n_half, row_tile, stop=True)
+            for n_half, row_tile in banks:
+                biased = opool.tile([P, BANK], F32, name="biased", align_bytes=64)
+                result = opool.tile([P, BANK], F32, name="result", align_bytes=64)
+                width = BANK // 2 if (n_half, row_tile) == banks[-1] else BANK
+                for c0 in range(0, BANK, width):
+                    cols, n0 = slice(c0, c0 + width), n_half * BANK + c0
+                    nc.vector.tensor_tensor(out=biased[:, cols], in0=acc[n_half, row_tile][:, cols],
+                                            in1=bf1_all[:, n0:n0 + width], op=ALU.add)
+                    nc.scalar.activation(out=result[:, cols], in_=biased[:, cols], func=ACT.Relu)
+                    nc.sync.dma_start(out=out[row_tile * P:(row_tile + 1) * P, n0:n0 + width], in_=result[:, cols])

from contextlib import ExitStack

import concourse.mybir as mybir
from concourse.masks import make_identity

BRANCHES, D_IN, D_OUT, ROWS = 8, 1024, 1024, 256
EPS = 1e-5
FLOPS = 2 * ROWS * BRANCHES * D_OUT * (D_IN + D_OUT)

F32 = mybir.dt.float32
BF16 = mybir.dt.bfloat16
U32 = mybir.dt.uint32
U8 = mybir.dt.uint8
FP8 = mybir.dt.float8_e4m3fn
FP8X4 = mybir.dt.float8_e4m3fn_x4
ACT = mybir.ActivationFunctionType
ALU = mybir.AluOpType
ENG = mybir.EngineType

P = 128
SLOTS = 4
K_PASS = P * SLOTS
PASSES_1 = D_IN // K_PASS
BANK = 512

OTHER_BLOCKS = ((1, 1), (1, 1), (2, 2), (2, 2), (2, 2), (2, 2), (2, 2), (2, 1))


def vector_slots(i, half):
    if i == 0:
        return (2, 3) if half == 0 else ()
    return (3,) if half == 1 and i % 2 == 1 else (2, 3)


def tile_extremeoptimizationlayer_pa_kernel(tc, x, W, b, gamma, beta, Wf1_bytes, Wf1_scale, bf1, out):
    nc = tc.nc
    with ExitStack() as ctx:
        keep = ctx.enter_context(tc.tile_pool(name="keep", bufs=1))
        wpool = ctx.enter_context(tc.tile_pool(name="wpool", bufs=1))
        fpool = ctx.enter_context(tc.tile_pool(name="fpool", bufs=1))
        hpool = ctx.enter_context(tc.tile_pool(name="hpool", bufs=1))
        opool = ctx.enter_context(tc.tile_pool(name="opool", bufs=4))
        acc_pool = ctx.enter_context(tc.psum_pool(name="acc_pool", bufs=1))
        ps1_pool = ctx.enter_context(tc.psum_pool(name="ps1_pool", bufs=2))
        inter_pool = ctx.enter_context(tc.psum_pool(name="inter_pool", bufs=2))

        w_raw, w_mix, w_codes, w_scales, w_bank = {}, {}, {}, {}, {}
        f_bytes, f_wide, f_mix, f_codes, f_scales = {}, {}, {}, {}, {}
        act, act_bank, normed, u_mix, u_codes, u_scales = {}, {}, {}, {}, {}, {}
        stat = {}


        def load_w(i, kp):
            w_raw[i, kp] = wpool.tile([P, SLOTS, D_OUT], BF16, name="w_raw", bufs=4, align_bytes=64)
            rows = W[i, kp * K_PASS:(kp + 1) * K_PASS, :]
            nc.sync.dma_start(out=w_raw[i, kp][:], in_=rows.rearrange("(p t) n -> p t n", t=SLOTS))

        def load_f(i, half):
            row0 = i * D_OUT + half * K_PASS
            f_bytes[i, half] = fpool.tile([P, SLOTS, D_OUT], U8, name="f_bytes", bufs=5, align_bytes=64)
            nc.sync.dma_start(out=f_bytes[i, half][:],
                              in_=Wf1_bytes[row0:row0 + K_PASS, :].rearrange("(p t) n -> p t n", t=SLOTS))


        def w_mix_of(i, kp):
            if (i, kp) not in w_mix:
                w_mix[i, kp] = wpool.tile([P, 2, SLOTS, P, SLOTS], BF16, name="w_mix", bufs=3, align_bytes=64)
            return w_mix[i, kp]

        def w_half(i, kp, half):
            return w_raw[i, kp][:, :, half * K_PASS:(half + 1) * K_PASS]

        def w_interleave(i, kp):
            tiles = 2 * (4 - OTHER_BLOCKS[i][kp])
            for half in range(2):
                slots = min(SLOTS, tiles - SLOTS * half)
                if slots > 0:
                    nc.vector.tensor_copy(
                        out=w_mix_of(i, kp)[:, half, 0:slots].rearrange("p q (c m) t -> p c q m t", m=2),
                        in_=w_half(i, kp, half).rearrange("p t (c m q) -> p c q m t", m=2, q=SLOTS)[:, :, 0:slots])

        def scalar_interleave(i, kp):
            for s in (2, 3):
                nc.scalar.copy(out=w_mix_of(i, kp)[:, 1, s],
                               in_=w_half(i, kp, 1).rearrange("p t (m q) -> p q m t", q=SLOTS)[:, s])

        def block_place(i, kp, blk):
            return divmod(2 * (4 - OTHER_BLOCKS[i][kp] + blk), SLOTS)

        def tensor_interleave(i, kp, blk):
            half, s0 = block_place(i, kp, blk)
            bank = inter_pool.tile([P, 2, P, SLOTS], BF16, name="inter_bank", tag="inter")
            w_bank[i, kp, blk] = bank
            moving = w_half(i, kp, half).rearrange("p t (m q) -> p q m t", q=SLOTS)
            for u in range(2):
                nc.tensor.matmul(out=bank[:, u].rearrange("p m t -> p (m t)"), lhsT=ident_b[:],
                                 rhs=moving[:, s0 + u], start=True, stop=True)

        def tensor_block_out(i, kp, blk):
            half, s0 = block_place(i, kp, blk)
            nc.scalar.copy(out=w_mix_of(i, kp)[:, half, s0:s0 + 2].rearrange("p s m t -> p (s m t)"),
                           in_=w_bank[i, kp, blk][:].rearrange("p s m t -> p (s m t)"))

        def tensor_blocks(i, kp):
            return range(OTHER_BLOCKS[i][kp] if i > 0 else 0)

        def w_quant(i, kp):
            w_codes[i, kp] = wpool.tile([P, D_OUT], U32, name="w_codes", bufs=4, align_bytes=64)
            w_scales[i, kp] = wpool.tile([P, D_OUT], U8, name="w_scales", bufs=4, align_bytes=64)
            nc.vector.quantize_mx(out=w_codes[i, kp][:].bitcast(FP8X4), scales=w_scales[i, kp][:],
                                  in_=w_mix[i, kp][:].rearrange("p h s m t -> p (h s m t)"))


        def f_widen(i, half, slots):
            if (i, half) not in f_wide:
                f_wide[i, half] = fpool.tile([P, SLOTS, D_OUT], BF16, name="f_wide", bufs=4, align_bytes=64)
            for t in slots:
                wide, byte = f_wide[i, half][:, t, :], f_bytes[i, half][:, t, :].bitcast(FP8)
                scale = f_row_scale[:, t, 2 * i + half:2 * i + half + 1]
                if t in vector_slots(i, half):
                    nc.vector.tensor_scalar(out=wide, in0=byte, scalar1=scale, scalar2=None, op0=ALU.mult)
                else:
                    nc.scalar.activation(out=wide, in_=byte, func=ACT.Copy, scale=scale)

        def f_interleave(i, half, c0=0, c1=D_OUT):
            if c0 == 0:
                f_mix[i, half] = fpool.tile([P, SLOTS * D_OUT], BF16, name="f_mix", bufs=2, align_bytes=64)
            nc.vector.tensor_copy(
                out=f_mix[i, half][:, SLOTS * c0:SLOTS * c1].rearrange("p (c m t) -> p c t m", m=4, t=SLOTS),
                in_=f_wide[i, half][:, :, c0:c1].rearrange("p t (c m) -> p c t m", m=4))

        def f_quant(i, half, c0=0, c1=D_OUT):
            if c0 == 0:
                f_codes[i, half] = fpool.tile([P, D_OUT], U32, name="f_codes", bufs=4, align_bytes=64)
                f_scales[i, half] = fpool.tile([P, D_OUT], U8, name="f_scales", bufs=4, align_bytes=64)
            nc.vector.quantize_mx(out=f_codes[i, half][:, c0:c1].bitcast(FP8X4), scales=f_scales[i, half][:, c0:c1],
                                  in_=f_mix[i, half][:, SLOTS * c0:SLOTS * c1])


        def stage1(i, pair):
            half, s0 = divmod(2 * pair, SLOTS)
            bank = ps1_pool.tile([P, 2, ROWS], F32, name="act_bank", tag="ps1")
            act_bank[i, pair] = bank
            for u in range(2):
                col0 = (half * SLOTS + s0 + u) * P
                cols = slice(col0, col0 + P)
                for kp in range(PASSES_1):
                    rows = slice(kp * ROWS, (kp + 1) * ROWS)
                    nc.tensor.matmul_mx(out=bank[:, u, :],
                                        lhsT=w_codes[i, kp][:, cols].bitcast(FP8X4), lhsT_scale=w_scales[i, kp][:, cols],
                                        rhs=x_codes[:, rows].bitcast(FP8X4), rhs_scale=x_scales[:, rows],
                                        start=(kp == 0), stop=(kp == PASSES_1 - 1))

        def stat_tile(i, name):
            stat[i, name] = hpool.tile([P, SLOTS, 2], F32, name="stat_" + name, bufs=2)
            return stat[i, name]

        def relu(i, pair):
            half, s0 = divmod(2 * pair, SLOTS)
            if pair == 0:
                stat_tile(i, "sum")
            if s0 == 0:
                act[i, half] = hpool.tile([P, SLOTS, ROWS], F32, name="act", bufs=4, align_bytes=64)
            for s in (s0, s0 + 1):
                nc.scalar.activation(out=act[i, half][:, s, :], in_=act_bank[i, pair][:, s - s0, :], func=ACT.Relu,
                                     bias=params[:, s, 2 * i + half:2 * i + half + 1],
                                     accum_out=stat[i, "sum"][:, s, half:half + 1])

        def neg_mean(i):
            nc.scalar.activation(out=stat_tile(i, "neg_mean")[:], in_=stat[i, "sum"][:], func=ACT.Copy, scale=-1.0 / ROWS)

        def squares(i):
            sums = stat_tile(i, "squares")
            for half in range(2):
                for s in range(SLOTS):
                    square = hpool.tile([P, ROWS], BF16, name="square", bufs=2)
                    nc.scalar.activation(out=square[:], in_=act[i, half][:, s, :], func=ACT.Square,
                                         bias=stat[i, "neg_mean"][:, s, half:half + 1], accum_out=sums[:, s, half:half + 1])

        def std(i):
            nc.scalar.activation(out=stat_tile(i, "std")[:], in_=stat[i, "squares"][:], func=ACT.Sqrt,
                                 scale=1.0 / ROWS, bias=EPS)

        def inv_std(i):
            nc.vector.reciprocal(out=stat_tile(i, "inv_std")[:], in_=stat[i, "std"][:])

        def norm_scale(i):
            nc.vector.tensor_tensor(out=stat_tile(i, "scale")[:], in0=stat[i, "inv_std"][:],
                                    in1=params[:, :, 16 + 2 * i:18 + 2 * i], op=ALU.mult)

        def norm_offset(i):
            nc.vector.tensor_tensor(out=stat_tile(i, "offset")[:], in0=stat[i, "neg_mean"][:], in1=stat[i, "scale"][:],
                                    op=ALU.mult)

        def norm_shift(i):
            nc.vector.tensor_tensor(out=stat_tile(i, "shift")[:], in0=stat[i, "offset"][:],
                                    in1=params[:, :, 32 + 2 * i:34 + 2 * i], op=ALU.add)


        def normalise(i, half, engine):
            if half == 0:
                normed[i] = hpool.tile([P, SLOTS, 2 * ROWS], BF16, name="normed", bufs=2, align_bytes=64)
            for s in range(SLOTS):
                result, a = normed[i][:, s, half * ROWS:(half + 1) * ROWS], act[i, half][:, s, :]
                scale, shift = stat[i, "scale"][:, s, half:half + 1], stat[i, "shift"][:, s, half:half + 1]
                if engine is nc.vector:
                    engine.tensor_scalar(out=result, in0=a, scalar1=scale, scalar2=shift, op0=ALU.mult, op1=ALU.add)
                else:
                    engine.activation(out=result, in_=a, func=ACT.Identity, scale=scale, bias=shift)

        def u_interleave(i, half0, half1):
            if i not in u_mix:
                u_mix[i] = hpool.tile([P, 2 * ROWS * SLOTS], BF16, name="u_mix", bufs=2, align_bytes=64)
            r0, r1 = half0 * ROWS, half1 * ROWS
            nc.vector.tensor_copy(
                out=u_mix[i][:, SLOTS * r0:SLOTS * r1].rearrange("p (c m t) -> p c t m", m=4, t=SLOTS),
                in_=normed[i][:, :, r0:r1].rearrange("p t (c m) -> p c t m", m=4))

        def u_quant(i, half0, half1):
            if i not in u_codes:
                u_codes[i] = hpool.tile([P, 2 * ROWS], U32, name="u_codes", bufs=2, align_bytes=64)
                u_scales[i] = hpool.tile([P, 2 * ROWS], U8, name="u_scales", bufs=2, align_bytes=64)
            r0, r1 = half0 * ROWS, half1 * ROWS
            nc.vector.quantize_mx(out=u_codes[i][:, r0:r1].bitcast(FP8X4), scales=u_scales[i][:, r0:r1],
                                  in_=u_mix[i][:, SLOTS * r0:SLOTS * r1])


        def stage2(i, half, n_half, row_tile, stop=False):
            rows = slice(half * ROWS + row_tile * P, half * ROWS + (row_tile + 1) * P)
            cols = slice(n_half * BANK, (n_half + 1) * BANK)
            nc.tensor.matmul_mx(out=acc[n_half, row_tile][:],
                                lhsT=u_codes[i][:, rows].bitcast(FP8X4), lhsT_scale=u_scales[i][:, rows],
                                rhs=f_codes[i, half][:, cols].bitcast(FP8X4), rhs_scale=f_scales[i, half][:, cols],
                                start=(i == 0 and half == 0), stop=stop)


        param_rows = keep.tile([P, K_PASS], BF16, name="param_rows", align_bytes=64)
        scale_rows = keep.tile([P, K_PASS], F32, name="scale_rows", align_bytes=64)
        ident_f = keep.tile([P, P], F32, name="ident_f", align_bytes=64)
        ident_b = keep.tile([P, P], BF16, name="ident_b", align_bytes=64)
        one = keep.tile([P, 1], F32, name="one")
        warm = keep.tile([P, 1], F32, name="warm")
        f_row_scale = keep.tile([P, SLOTS, 16], F32, name="f_row_scale")
        params = keep.tile([P, SLOTS, 48], F32, name="params")
        x_rows = keep.tile([P, 2, D_IN], BF16, name="x_rows", align_bytes=64)
        x_mix = keep.tile([P, PASSES_1, ROWS * SLOTS], BF16, name="x_mix", align_bytes=64)
        x_codes = keep.tile([P, PASSES_1 * ROWS], U32, name="x_codes", align_bytes=64)
        x_scales = keep.tile([P, PASSES_1 * ROWS], U8, name="x_scales", align_bytes=64)
        bf1_all = keep.tile([P, D_OUT], BF16, name="bf1_all", align_bytes=64)
        acc = {}
        for n_half in range(2):
            for row_tile in range(2):
                acc[n_half, row_tile] = acc_pool.tile([P, BANK], F32, name="acc" + str(2 * n_half + row_tile))

        nc.vector.memset(scale_rows[:], 0.0)
        nc.vector.memset(param_rows[:], 0.0)
        nc.vector.memset(one[:], 1.0)
        make_identity(nc, ident_f[:])
        make_identity(nc, ident_b[:])
        nc.scalar.dma_start(out=scale_rows[0:16, :], in_=Wf1_scale.rearrange("(s c) o -> s (o c)", c=K_PASS))
        load_f(0, 0)
        for n, vector in enumerate((b, gamma, beta)):
            nc.scalar.dma_start(out=param_rows[16 * n:16 * (n + 1), :], in_=vector.rearrange("k (h c) -> (k h) c", c=K_PASS))
        load_w(0, 0)
        load_f(0, 1)
        for row_tile in range(2):
            nc.sync.dma_start(out=x_rows[:, row_tile, :], in_=x[row_tile * P:(row_tile + 1) * P, :])
        load_w(0, 1)
        nc.scalar.activation(out=warm[:], in_=one[:], func=ACT.Sqrt)

        with tc.manual_schedule(engines={ENG.PE, ENG.Activation, ENG.DVE, ENG.SP}):
            bank = ps1_pool.tile([P, SLOTS, P], F32, name="scale_bank", tag="ps1")
            for t in range(SLOTS):
                nc.tensor.transpose(bank[:, t, :], scale_rows[:, t:K_PASS:SLOTS], ident_f[:])
            nc.scalar.copy(out=f_row_scale[:], in_=bank[:, :, 0:16])
            f_widen(0, 0, range(SLOTS))
            scalar_interleave(0, 0)
            f_widen(0, 1, (0, 1))

            for kp in range(PASSES_1):
                bank = ps1_pool.tile([P, 2, ROWS], F32, name="x_bank", tag="ps1")
                words = slice(kp * K_PASS // 2, (kp + 1) * K_PASS // 2)
                for row_tile in range(2):
                    for u in range(2):
                        nc.tensor.transpose(bank[:, u, row_tile * P:(row_tile + 1) * P],
                                            x_rows[:, row_tile, :].bitcast(F32)[:, words][:, u::2], ident_f[:])
                nc.scalar.copy(out=x_mix[:, kp, :].bitcast(F32).rearrange("p (r u) -> p r u", u=2),
                               in_=bank[:].rearrange("p u r -> p r u"))

            scalar_interleave(0, 1)
            f_widen(0, 1, (2, 3))
            bank = inter_pool.tile([P, SLOTS, P], BF16, name="param_bank", tag="inter")
            for s in range(SLOTS):
                nc.tensor.transpose(bank[:, s, :], param_rows[:, s:K_PASS:SLOTS], ident_b[:])
            nc.scalar.copy(out=params[:], in_=bank[:, :, 0:48])

            for i in range(-1, BRANCHES):
                cur, nxt, nxt2 = i >= 0, i + 1 < BRANCHES, i + 2 < BRANCHES
                if nxt2:
                    for half in range(2):
                        load_w(i + 2, half)
                        load_f(i + 2, half)
                if i == 1:
                    nc.sync.dma_start(out=bf1_all[:], in_=bf1.partition_broadcast(P))

                if cur:
                    stage1(i, 0)
                    stage1(i, 1)
                if nxt:
                    w_interleave(i + 1, 0)
                for pair in range(4):
                    if cur:
                        if pair >= 2:
                            stage1(i, pair)
                        relu(i, pair)
                    if nxt and pair in tensor_blocks(i + 1, 0):
                        tensor_block_out(i + 1, 0, pair)
                if cur:
                    f_interleave(i, 0, BANK if i == 0 else 0)
                if nxt:
                    for blk in tensor_blocks(i + 1, 1):
                        tensor_interleave(i + 1, 1, blk)
                if i > 0:
                    for half in range(2):
                        for n_half in range(2):
                            for row_tile in range(2):
                                stage2(i - 1, half, n_half, row_tile)
                if cur:
                    neg_mean(i)
                    squares(i)
                    std(i)
                if nxt:
                    for blk in tensor_blocks(i + 1, 1):
                        tensor_block_out(i + 1, 1, blk)
                    w_quant(i + 1, 0)
                    if not cur:
                        f_interleave(0, 0, 0, BANK)
                    w_interleave(i + 1, 1)
                if not cur:
                    nc.vector.quantize_mx(out=x_codes[:].bitcast(FP8X4), scales=x_scales[:],
                                          in_=x_mix[:].rearrange("p k c -> p (k c)"))

                if cur and nxt:
                    f_quant(i, 0)
                    inv_std(i)
                    f_widen(i + 1, 0, (3, 0, 1))
                    norm_scale(i)
                    f_widen(i + 1, 0, (2,))
                    norm_offset(i)
                    f_widen(i + 1, 1, vector_slots(i + 1, 1))
                    norm_shift(i)
                elif cur:
                    f_interleave(i, 1)
                    f_quant(i, 0)
                    inv_std(i)
                    f_quant(i, 1, 0, BANK)
                    norm_scale(i)
                    f_quant(i, 1, BANK, D_OUT)
                    norm_offset(i)
                    norm_shift(i)
                if nxt2:
                    for blk in tensor_blocks(i + 2, 0):
                        tensor_interleave(i + 2, 0, blk)
                if cur and nxt:
                    normalise(i, 0, nc.scalar)
                    normalise(i, 1, nc.scalar)
                    w_quant(i + 1, 1)
                    f_widen(i + 1, 1, [t for t in range(SLOTS) if t not in vector_slots(i + 1, 1)])
                    f_interleave(i, 1)
                    u_interleave(i, 0, 2)
                    f_quant(i, 1)
                    u_quant(i, 0, 2)
                elif cur:
                    normalise(i, 0, nc.scalar)
                    normalise(i, 1, nc.vector)
                    u_interleave(i, 1, 2)
                    u_interleave(i, 0, 1)
                    u_quant(i, 1, 2)
                    u_quant(i, 0, 1)
                else:
                    w_quant(0, 1)

            banks = [(n_half, row_tile) for n_half in range(2) for row_tile in range(2)]
            for n_half, row_tile in banks:
                stage2(BRANCHES - 1, 1, n_half, row_tile)
                stage2(BRANCHES - 1, 0, n_half, row_tile, stop=True)
            for n_half, row_tile in banks:
                biased = opool.tile([P, BANK], F32, name="biased", align_bytes=64)
                result = opool.tile([P, BANK], F32, name="result", align_bytes=64)
                width = BANK // 2 if (n_half, row_tile) == banks[-1] else BANK
                for c0 in range(0, BANK, width):
                    cols, n0 = slice(c0, c0 + width), n_half * BANK + c0
                    nc.vector.tensor_tensor(out=biased[:, cols], in0=acc[n_half, row_tile][:, cols],
                                            in1=bf1_all[:, n0:n0 + width], op=ALU.add)
                    nc.scalar.activation(out=result[:, cols], in_=biased[:, cols], func=ACT.Relu)
                    nc.sync.dma_start(out=out[row_tile * P:(row_tile + 1) * P, n0:n0 + width], in_=result[:, cols])
